import numpy as np
import ml_dtypes


def mxq(x, axis, fmt="e4m3"):
    dtype, down = {"e4m3": (ml_dtypes.float8_e4m3fn, 7), "e5m2": (ml_dtypes.float8_e5m2, 14)}[fmt]
    v = np.moveaxis(np.asarray(x, np.float32).astype(ml_dtypes.bfloat16).astype(np.float64), axis, -1)
    blocks = v.reshape(v.shape[:-1] + (-1, 32))
    amax = np.abs(blocks).max(-1, keepdims=True)
    byte = np.maximum(np.where(amax > 0, np.frexp(amax)[1] - 1 + 127, 0) - down, 1)
    scale = np.exp2(byte - 127.0)
    codes = (blocks / scale).astype(np.float32).astype(dtype).astype(np.float64)
    return np.moveaxis((codes * scale).reshape(v.shape), -1, axis)


WIDE = False


def mx_kscale(k):
    if not WIDE:
        return np.ones(k)
    levels = np.array([10, -10, 5, -5, 0])
    a = np.random.permutation(np.resize(levels, k // 512 * 4)).reshape(k // 512, 4)
    idx = np.arange(k)
    return np.exp2(a[idx // 512, idx % 128 // 32])


BF16 = ml_dtypes.bfloat16


def bf(x):
    return np.asarray(x, np.float32).astype(BF16)


def f64(x):
    return np.asarray(x).astype(np.float64)


B, N, D, H, DK, DV = 4, 4096, 512, 4, 64, 64


def xnorm(x, g):
    n = np.sqrt(np.sum(x * x, axis=-1, keepdims=True))
    return x * g / n


def setup_inputs():
    s = mx_kscale(D)
    return {
        "queries": bf(np.random.standard_normal((B, N, D)) * s),
        "Wk": bf(np.random.standard_normal((D, H * DK)) * 0.5 / np.sqrt(D) / s[:, None]),
        "bk": bf(np.random.standard_normal(H * DK) * 0.05),
        "Wv": bf(np.random.standard_normal((D, H * DV)) * 0.5 / np.sqrt(D) / s[:, None]),
        "bv": bf(np.random.standard_normal(H * DV) * 0.05),
        "gamma": bf(np.random.standard_normal((1, H, 1, 1)) * 2.0),
    }


def reference(queries, Wk, bk, Wv, bv, gamma):
    xq = mxq(f64(queries), 2, "e4m3")
    k = ((xq @ mxq(f64(Wk), 0, "e4m3")) + f64(bk)).reshape(B, N, H, DK)
    v = ((xq @ mxq(f64(Wv), 0, "e4m3")) + f64(bv)).reshape(B, N, H, DV)
    kv = mxq(k.transpose(0, 2, 3, 1), 3, "e4m3") @ mxq(v.transpose(0, 2, 1, 3), 2, "e4m3")
    return xnorm(kv, f64(gamma))

@@ -1,0 +1,254 @@
+from contextlib import ExitStack
+
+import concourse.mybir as mybir
+from concourse.masks import make_identity
+
+BF16 = mybir.dt.bfloat16
+F32 = mybir.dt.float32
+U32 = mybir.dt.uint32
+U8 = mybir.dt.uint8
+FP8X4 = mybir.dt.float8_e4m3fn_x4
+ADD = mybir.AluOpType.add
+MULT = mybir.AluOpType.mult
+ACT = mybir.ActivationFunctionType
+
+BATCHES, TOKENS_PER_BATCH, FEATURES, HEADS, HEAD_DIM = 4, 4096, 512, 4, 64
+
+P = 128
+PACK = 4
+GROUP = P * PACK
+GROUPS = BATCHES * TOKENS_PER_BATCH // GROUP
+GROUPS_PER_BATCH = TOKENS_PER_BATCH // GROUP
+KEY_COLS = HEADS * HEAD_DIM
+COLS = 2 * KEY_COLS
+BLOCK = P
+BLOCKS = COLS // BLOCK
+HEAD_PAIRS = HEADS // 2
+WORDS = FEATURES // 2
+X_BUFS = 8
+
+FLOPS = 2 * BATCHES * TOKENS_PER_BATCH * (FEATURES * COLS + HEADS * HEAD_DIM * HEAD_DIM)
+
+
+def tile_ufoattention_pa_t_kernel(tc, queries, Wk, bk, Wv, bv, gamma, out):
+    nc = tc.nc
+    tokens = queries.flatten_outer_dims()
+
+    with ExitStack() as ctx:
+        consts = ctx.enter_context(tc.tile_pool(name="consts", bufs=1))
+        x_pool = ctx.enter_context(tc.tile_pool(name="x", bufs=X_BUFS))
+        work = ctx.enter_context(tc.tile_pool(name="work", bufs=2))
+        xt_pool = ctx.enter_context(tc.psum_pool(name="xt", bufs=2))
+        proj_pool = ctx.enter_context(tc.psum_pool(name="proj", bufs=BLOCKS))
+        kv_pool = ctx.enter_context(tc.psum_pool(name="kv", bufs=1))
+        ctx.enter_context(tc.manual_schedule())
+
+        x_tiles = {}
+        x_grouped = {}
+        x_mx = {}
+        proj_banks = {}
+        kv_grouped = {}
+        kv_mx = {}
+        kv_sums = {}
+
+        def load(g):
+            x_sb = x_pool.tile([P, PACK * FEATURES], BF16)
+            nc.sync.dma_start(
+                out=x_sb[:],
+                in_=tokens[g * GROUP : (g + 1) * GROUP, :].rearrange("(p t) d -> p (t d)", t=PACK),
+            )
+            x_tiles[g] = x_sb
+
+        def transpose(g):
+            x_words = x_tiles[g][:].bitcast(F32)
+            grouped = work.tile([P, GROUP * PACK], BF16, align_bytes=64, name="x_grouped")
+            grouped_words = grouped[:].bitcast(F32)
+            for bank in range(2):
+                xt = xt_pool.tile([P, 2, 2, P], F32)
+                for s in range(2):
+                    for u in range(2):
+                        first = ((2 * bank + s) * 2 + u) * P
+                        nc.tensor.transpose(xt[:, s, u, :], x_words[:, first : first + P], ident[:])
+                nc.scalar.copy(
+                    out=grouped_words[:, bank * 4 * P : (bank + 1) * 4 * P].rearrange(
+                        "q (s p u) -> q s p u", s=2, u=2
+                    ),
+                    in_=xt[:].rearrange("q s u p -> q s p u"),
+                )
+            x_grouped[g] = grouped
+
+        def quantise_x(g):
+            words = work.tile([P, GROUP], U32, align_bytes=64, name="x_words")
+            scales = work.tile([P, GROUP], U8, align_bytes=64, name="x_scales")
+            nc.vector.quantize_mx(out=words[:].bitcast(FP8X4), scales=scales[:], in_=x_grouped[g][:])
+            x_mx[g] = (words, scales)
+
+        def project(g, block):
+            words, scales = x_mx[g]
+            cols = slice(block * BLOCK, (block + 1) * BLOCK)
+            bank = proj_pool.tile([P, PACK, BLOCK], F32, name="proj_bank")
+            for t in range(PACK):
+                slot = slice(t * P, (t + 1) * P)
+                nc.tensor.matmul_mx(
+                    out=bank[:, t, :],
+                    lhsT=words[:, slot].bitcast(FP8X4),
+                    lhsT_scale=scales[:, slot],
+                    rhs=w_words[:, cols].bitcast(FP8X4),
+                    rhs_scale=w_scales[:, cols],
+                    start=True,
+                    stop=True,
+                )
+            proj_banks[(g, block)] = bank
+
+        def add_bias(g, block):
+            if block == 0:
+                kv_grouped[g] = work.tile([P, COLS, PACK], BF16, align_bytes=64, name="kv_grouped")
+            cols = slice(block * BLOCK, (block + 1) * BLOCK)
+            nc.vector.tensor_tensor(
+                out=kv_grouped[g][:, cols, :],
+                in0=proj_banks[(g, block)][:].rearrange("p t c -> p c t"),
+                in1=bias[:, cols].unsqueeze(2).to_broadcast([P, BLOCK, PACK]),
+                op=ADD,
+            )
+
+        def quantise_kv(g):
+            words = work.tile([P, COLS], U32, align_bytes=64, name="kv_words")
+            scales = work.tile([P, COLS], U8, align_bytes=64, name="kv_scales")
+            nc.vector.quantize_mx(
+                out=words[:].bitcast(FP8X4),
+                scales=scales[:],
+                in_=kv_grouped[g][:].rearrange("p c t -> p (c t)"),
+            )
+            kv_mx[g] = (words, scales)
+
+        def accumulate(g):
+            words, scales = kv_mx[g]
+            step = g % GROUPS_PER_BATCH
+            for pair in range(HEAD_PAIRS):
+                if step == 0:
+                    kv_sums[pair] = kv_pool.tile([P, BLOCK], F32, name="kv_sum%d" % pair)
+                k_cols = slice(pair * BLOCK, (pair + 1) * BLOCK)
+                v_cols = slice(KEY_COLS + pair * BLOCK, KEY_COLS + (pair + 1) * BLOCK)
+                nc.tensor.matmul_mx(
+                    out=kv_sums[pair][:],
+                    lhsT=words[:, k_cols].bitcast(FP8X4),
+                    lhsT_scale=scales[:, k_cols],
+                    rhs=words[:, v_cols].bitcast(FP8X4),
+                    rhs_scale=scales[:, v_cols],
+                    start=(step == 0),
+                    stop=(step == GROUPS_PER_BATCH - 1),
+                )
+
+        def collect(b):
+            for pair in range(HEAD_PAIRS):
+                place = b * HEAD_PAIRS + pair
+                for half in range(2):
+                    rows = slice(half * HEAD_DIM, (half + 1) * HEAD_DIM)
+                    nc.scalar.copy(out=kv_all[rows, place, :], in_=kv_sums[pair][rows, rows])
+                nc.scalar.activation(
+                    out=squares[:],
+                    in_=kv_all[:, place, :],
+                    func=ACT.Square,
+                    accum_out=sum_squares[:, place : place + 1],
+                )
+
+        w_raw = consts.tile([P, 2, PACK, KEY_COLS], BF16)
+        for which, w in enumerate((Wk, Wv)):
+            nc.scalar.dma_start(
+                out=w_raw[:, which, :, :].rearrange("q (u e) c -> q u (e c)", u=2),
+                in_=w.rearrange("(u q e) c -> q u (e c)", u=2, e=2),
+            )
+        bias_row = consts.tile([P, COLS], BF16)
+        nc.vector.memset(bias_row[:], 0.0)
+        nc.scalar.dma_start(out=bias_row[0:1, 0:KEY_COLS], in_=bk.unsqueeze(0))
+        nc.scalar.dma_start(out=bias_row[0:1, KEY_COLS:COLS], in_=bv.unsqueeze(0))
+        for g in range(X_BUFS):
+            load(g)
+
+        ident = consts.tile([P, P], F32)
+        make_identity(nc, ident[:])
+        gamma_bf = consts.tile([P, HEADS], BF16)
+        nc.gpsimd.dma_start(
+            out=gamma_bf[:], in_=gamma.rearrange("o h x y -> (o h x y)").partition_broadcast(P)
+        )
+
+        one = consts.tile([P, 1], F32)
+        nc.vector.memset(one[:], 1.0)
+        warm = consts.tile([P, 1], F32)
+        nc.scalar.activation(out=warm[:], in_=one[:], func=ACT.Sqrt)
+
+        ones = consts.tile([P, P], BF16)
+        nc.vector.memset(ones[:], 1.0)
+        bias_bank = proj_pool.tile([P, COLS], F32, name="proj_bank")
+        nc.tensor.matmul(out=bias_bank[:], lhsT=ones[:], rhs=bias_row[:], start=True, stop=True)
+        bias = consts.tile([P, COLS], F32)
+        nc.scalar.copy(out=bias[:], in_=bias_bank[:])
+
+        w_grouped = consts.tile([P, COLS, PACK], BF16, align_bytes=64)
+        nc.vector.tensor_copy(
+            out=w_grouped[:].rearrange("q (w c) t -> q w c t", w=2),
+            in_=w_raw[:].rearrange("q w t c -> q w c t"),
+        )
+        w_words = consts.tile([P, COLS], U32, align_bytes=64)
+        w_scales = consts.tile([P, COLS], U8, align_bytes=64)
+        nc.vector.quantize_mx(
+            out=w_words[:].bitcast(FP8X4),
+            scales=w_scales[:],
+            in_=w_grouped[:].rearrange("q c t -> q (c t)"),
+        )
+
+        kv_all = consts.tile([P, BATCHES * HEAD_PAIRS, HEAD_DIM], F32)
+        squares = consts.tile([P, HEAD_DIM], F32)
+        sum_squares = consts.tile([P, BATCHES * HEAD_PAIRS], F32)
+
+        for i in range(-3, GROUPS):
+            for block in range(BLOCKS):
+                if i >= 0:
+                    add_bias(i, block)
+                if 0 <= i + 1 < GROUPS:
+                    project(i + 1, block)
+            if 0 <= i + 2 < GROUPS:
+                quantise_x(i + 2)
+            if i >= 0:
+                quantise_kv(i)
+            if i + 3 < GROUPS:
+                transpose(i + 3)
+                if i + 3 + X_BUFS < GROUPS:
+                    load(i + 3 + X_BUFS)
+            if i >= 0:
+                accumulate(i)
+                if i % GROUPS_PER_BATCH == GROUPS_PER_BATCH - 1:
+                    collect(i // GROUPS_PER_BATCH)
+
+        gamma_rows = consts.tile([P, HEAD_PAIRS], F32)
+        for half in range(2):
+            rows = slice(half * HEAD_DIM, (half + 1) * HEAD_DIM)
+            nc.vector.tensor_copy(
+                out=gamma_rows[rows, :],
+                in_=gamma_bf[rows, :].rearrange("p (pair half) -> p half pair", half=2)[:, half, :],
+            )
+        norms = consts.tile([P, BATCHES, HEAD_PAIRS], F32)
+        nc.scalar.activation(
+            out=norms[:].rearrange("p b pair -> p (b pair)"), in_=sum_squares[:], func=ACT.Sqrt
+        )
+        gains = consts.tile([P, BATCHES, HEAD_PAIRS], F32)
+        nc.vector.reciprocal(out=gains[:], in_=norms[:])
+        nc.vector.tensor_tensor(
+            out=gains[:],
+            in0=gains[:],
+            in1=gamma_rows[:].unsqueeze(1).to_broadcast([P, BATCHES, HEAD_PAIRS]),
+            op=MULT,
+        )
+        result = consts.tile([P, BATCHES * HEAD_PAIRS, HEAD_DIM], F32)
+        nc.vector.tensor_tensor(
+            out=result[:],
+            in0=kv_all[:],
+            in1=gains[:]
+            .rearrange("p b pair -> p (b pair)")
+            .unsqueeze(2)
+            .to_broadcast([P, BATCHES * HEAD_PAIRS, HEAD_DIM]),
+            op=MULT,
+        )
+        nc.sync.dma_start(
+            out=out.rearrange("b (pair half) i j -> (half i) (b pair) j", half=2), in_=result[:]
+        )

@@ -23,6 +23,7 @@ KEY_COLS = HEADS * HEAD_DIM
 COLS = 2 * KEY_COLS
 BLOCK = P
 BLOCKS = COLS // BLOCK
+VECTOR_BLOCKS = BLOCKS - 1
 HEAD_PAIRS = HEADS // 2
 WORDS = FEATURES // 2
 X_BUFS = 8
@@ -38,6 +39,7 @@ def tile_ufoattention_pa_t_kernel(tc, queries, Wk, bk, Wv, bv, gamma, out):
         consts = ctx.enter_context(tc.tile_pool(name="consts", bufs=1))
         x_pool = ctx.enter_context(tc.tile_pool(name="x", bufs=X_BUFS))
         work = ctx.enter_context(tc.tile_pool(name="work", bufs=2))
+        kv_grouped_pool = ctx.enter_context(tc.tile_pool(name="kv_grouped", bufs=1))
         xt_pool = ctx.enter_context(tc.psum_pool(name="xt", bufs=2))
         proj_pool = ctx.enter_context(tc.psum_pool(name="proj", bufs=BLOCKS))
         kv_pool = ctx.enter_context(tc.psum_pool(name="kv", bufs=1))
@@ -47,6 +49,7 @@ def tile_ufoattention_pa_t_kernel(tc, queries, Wk, bk, Wv, bv, gamma, out):
         x_grouped = {}
         x_mx = {}
         proj_banks = {}
+        staged = {}
         kv_grouped = {}
         kv_mx = {}
         kv_sums = {}
@@ -102,11 +105,28 @@ def tile_ufoattention_pa_t_kernel(tc, queries, Wk, bk, Wv, bv, gamma, out):
 
         def add_bias(g, block):
             if block == 0:
-                kv_grouped[g] = work.tile([P, COLS, PACK], BF16, align_bytes=64, name="kv_grouped")
+                kv_grouped[g] = kv_grouped_pool.tile(
+                    [P, COLS, PACK], BF16, align_bytes=64, name="kv_grouped"
+                )
             cols = slice(block * BLOCK, (block + 1) * BLOCK)
             nc.vector.tensor_tensor(
                 out=kv_grouped[g][:, cols, :],
                 in0=proj_banks[(g, block)][:].rearrange("p t c -> p c t"),
+                in1=bias[:, cols].unsqueeze(2).to_broadcast([P, BLOCK, PACK]),
+                op=ADD,
+            )
+
+        def stage_last_block(g):
+            staged[g] = work.tile([P, BLOCK, PACK], F32, name="staged")
+            nc.scalar.copy(
+                out=staged[g][:], in_=proj_banks[(g, VECTOR_BLOCKS)][:].rearrange("p t c -> p c t")
+            )
+
+        def add_bias_to_last_block(g):
+            cols = slice(VECTOR_BLOCKS * BLOCK, COLS)
+            nc.gpsimd.tensor_tensor(
+                out=kv_grouped[g][:, cols, :],
+                in0=staged[g][:],
                 in1=bias[:, cols].unsqueeze(2).to_broadcast([P, BLOCK, PACK]),
                 op=ADD,
             )
@@ -202,11 +222,16 @@ def tile_ufoattention_pa_t_kernel(tc, queries, Wk, bk, Wv, bv, gamma, out):
         sum_squares = consts.tile([P, BATCHES * HEAD_PAIRS], F32)
 
         for i in range(-3, GROUPS):
-            for block in range(BLOCKS):
+            if 0 <= i + 1 < GROUPS:
+                project(i + 1, VECTOR_BLOCKS)
+                stage_last_block(i + 1)
+            for block in range(VECTOR_BLOCKS):
                 if i >= 0:
                     add_bias(i, block)
                 if 0 <= i + 1 < GROUPS:
                     project(i + 1, block)
+            if i >= 0:
+                add_bias_to_last_block(i)
             if 0 <= i + 2 < GROUPS:
                 quantise_x(i + 2)
             if i >= 0:

@@ -24,6 +24,7 @@ COLS = 2 * KEY_COLS
 BLOCK = P
 BLOCKS = COLS // BLOCK
 VECTOR_BLOCKS = BLOCKS - 1
+LAST_COLS = slice(VECTOR_BLOCKS * BLOCK, COLS)
 HEAD_PAIRS = HEADS // 2
 WORDS = FEATURES // 2
 X_BUFS = 8
@@ -39,9 +40,10 @@ def tile_ufoattention_pa_t_kernel(tc, queries, Wk, bk, Wv, bv, gamma, out):
         consts = ctx.enter_context(tc.tile_pool(name="consts", bufs=1))
         x_pool = ctx.enter_context(tc.tile_pool(name="x", bufs=X_BUFS))
         work = ctx.enter_context(tc.tile_pool(name="work", bufs=2))
-        kv_grouped_pool = ctx.enter_context(tc.tile_pool(name="kv_grouped", bufs=1))
-        xt_pool = ctx.enter_context(tc.psum_pool(name="xt", bufs=2))
-        proj_pool = ctx.enter_context(tc.psum_pool(name="proj", bufs=BLOCKS))
+        batch_pool = ctx.enter_context(tc.tile_pool(name="batch", bufs=2))
+        xt_pool = ctx.enter_context(tc.psum_pool(name="xt", bufs=3))
+        proj_pool = ctx.enter_context(tc.psum_pool(name="proj", bufs=VECTOR_BLOCKS))
+        last_pool = ctx.enter_context(tc.psum_pool(name="last", bufs=1))
         kv_pool = ctx.enter_context(tc.psum_pool(name="kv", bufs=1))
         ctx.enter_context(tc.manual_schedule())
 
@@ -49,10 +51,10 @@ def tile_ufoattention_pa_t_kernel(tc, queries, Wk, bk, Wv, bv, gamma, out):
         x_grouped = {}
         x_mx = {}
         proj_banks = {}
-        staged = {}
+        last_banks = {}
+        last_rounded = {}
         kv_grouped = {}
         kv_mx = {}
-        kv_sums = {}
 
         def load(g):
             x_sb = x_pool.tile([P, PACK * FEATURES], BF16)
@@ -67,7 +69,7 @@ def tile_ufoattention_pa_t_kernel(tc, queries, Wk, bk, Wv, bv, gamma, out):
             grouped = work.tile([P, GROUP * PACK], BF16, align_bytes=64, name="x_grouped")
             grouped_words = grouped[:].bitcast(F32)
             for bank in range(2):
-                xt = xt_pool.tile([P, 2, 2, P], F32)
+                xt = xt_pool.tile([P, 2, 2, P], F32, name="xt", tag="xt")
                 for s in range(2):
                     for u in range(2):
                         first = ((2 * bank + s) * 2 + u) * P
@@ -104,10 +106,6 @@ def tile_ufoattention_pa_t_kernel(tc, queries, Wk, bk, Wv, bv, gamma, out):
             proj_banks[(g, block)] = bank
 
         def add_bias(g, block):
-            if block == 0:
-                kv_grouped[g] = kv_grouped_pool.tile(
-                    [P, COLS, PACK], BF16, align_bytes=64, name="kv_grouped"
-                )
             cols = slice(block * BLOCK, (block + 1) * BLOCK)
             nc.vector.tensor_tensor(
                 out=kv_grouped[g][:, cols, :],
@@ -116,55 +114,76 @@ def tile_ufoattention_pa_t_kernel(tc, queries, Wk, bk, Wv, bv, gamma, out):
                 op=ADD,
             )
 
-        def stage_last_block(g):
-            staged[g] = work.tile([P, BLOCK, PACK], F32, name="staged")
-            nc.scalar.copy(
-                out=staged[g][:], in_=proj_banks[(g, VECTOR_BLOCKS)][:].rearrange("p t c -> p c t")
+        def project_last_block(g):
+            words, scales = x_mx[g]
+            bank = last_pool.tile([P, GROUP], F32, name="last_bank")
+            nc.tensor.matmul_mx(
+                out=bank[:],
+                lhsT=w_words[:, LAST_COLS].bitcast(FP8X4),
+                lhsT_scale=w_scales[:, LAST_COLS],
+                rhs=words[:].bitcast(FP8X4),
+                rhs_scale=scales[:],
+                start=True,
+                stop=True,
             )
+            last_banks[g] = bank
 
         def add_bias_to_last_block(g):
-            cols = slice(VECTOR_BLOCKS * BLOCK, COLS)
-            nc.gpsimd.tensor_tensor(
-                out=kv_grouped[g][:, cols, :],
-                in0=staged[g][:],
-                in1=bias[:, cols].unsqueeze(2).to_broadcast([P, BLOCK, PACK]),
-                op=ADD,
+            last_rounded[g] = work.tile([P, GROUP], BF16, name="last_rounded")
+            nc.scalar.activation(
+                out=last_rounded[g][:],
+                in_=last_banks[g][:],
+                func=ACT.Identity,
+                bias=last_bias[:, 0:1],
+                scale=1.0,
+            )
+
+        def transpose_last_block(g):
+            kv_grouped[g] = work.tile([P, COLS, PACK], BF16, align_bytes=64, name="kv_grouped")
+            back = xt_pool.tile([P, PACK, BLOCK], BF16, name="back", tag="xt")
+            for t in range(PACK):
+                nc.tensor.transpose(
+                    back[:, t, :], last_rounded[g][:, t * P : (t + 1) * P], ident_bf[:]
+                )
+            nc.scalar.copy(
+                out=kv_grouped[g][:, LAST_COLS, :], in_=back[:].rearrange("p t c -> p c t")
             )
 
         def quantise_kv(g):
-            words = work.tile([P, COLS], U32, align_bytes=64, name="kv_words")
-            scales = work.tile([P, COLS], U8, align_bytes=64, name="kv_scales")
+            b, step = divmod(g, GROUPS_PER_BATCH)
+            if step == 0:
+                kv_mx[b] = (
+                    batch_pool.tile([P, GROUPS_PER_BATCH, COLS], U32, align_bytes=64, name="kv_words"),
+                    batch_pool.tile([P, GROUPS_PER_BATCH, COLS], U8, align_bytes=64, name="kv_scales"),
+                )
+            words, scales = kv_mx[b]
             nc.vector.quantize_mx(
-                out=words[:].bitcast(FP8X4),
-                scales=scales[:],
+                out=words[:, step, :].bitcast(FP8X4),
+                scales=scales[:, step, :],
                 in_=kv_grouped[g][:].rearrange("p c t -> p (c t)"),
             )
-            kv_mx[g] = (words, scales)
 
-        def accumulate(g):
-            words, scales = kv_mx[g]
-            step = g % GROUPS_PER_BATCH
+        def second_product(b):
+            words, scales = kv_mx[b]
+            kv_sums = kv_pool.tile([P, HEAD_PAIRS, BLOCK], F32)
             for pair in range(HEAD_PAIRS):
-                if step == 0:
-                    kv_sums[pair] = kv_pool.tile([P, BLOCK], F32, name="kv_sum%d" % pair)
                 k_cols = slice(pair * BLOCK, (pair + 1) * BLOCK)
                 v_cols = slice(KEY_COLS + pair * BLOCK, KEY_COLS + (pair + 1) * BLOCK)
-                nc.tensor.matmul_mx(
-                    out=kv_sums[pair][:],
-                    lhsT=words[:, k_cols].bitcast(FP8X4),
-                    lhsT_scale=scales[:, k_cols],
-                    rhs=words[:, v_cols].bitcast(FP8X4),
-                    rhs_scale=scales[:, v_cols],
-                    start=(step == 0),
-                    stop=(step == GROUPS_PER_BATCH - 1),
-                )
-
-        def collect(b):
+                for step in range(GROUPS_PER_BATCH):
+                    nc.tensor.matmul_mx(
+                        out=kv_sums[:, pair, :],
+                        lhsT=words[:, step, k_cols].bitcast(FP8X4),
+                        lhsT_scale=scales[:, step, k_cols],
+                        rhs=words[:, step, v_cols].bitcast(FP8X4),
+                        rhs_scale=scales[:, step, v_cols],
+                        start=(step == 0),
+                        stop=(step == GROUPS_PER_BATCH - 1),
+                    )
             for pair in range(HEAD_PAIRS):
                 place = b * HEAD_PAIRS + pair
                 for half in range(2):
                     rows = slice(half * HEAD_DIM, (half + 1) * HEAD_DIM)
-                    nc.scalar.copy(out=kv_all[rows, place, :], in_=kv_sums[pair][rows, rows])
+                    nc.scalar.copy(out=kv_all[rows, place, :], in_=kv_sums[rows, pair, rows])
                 nc.scalar.activation(
                     out=squares[:],
                     in_=kv_all[:, place, :],
@@ -180,13 +199,15 @@ def tile_ufoattention_pa_t_kernel(tc, queries, Wk, bk, Wv, bv, gamma, out):
             )
         bias_row = consts.tile([P, COLS], BF16)
         nc.vector.memset(bias_row[:], 0.0)
-        nc.scalar.dma_start(out=bias_row[0:1, 0:KEY_COLS], in_=bk.unsqueeze(0))
-        nc.scalar.dma_start(out=bias_row[0:1, KEY_COLS:COLS], in_=bv.unsqueeze(0))
+        nc.sync.dma_start(out=bias_row[0:1, 0:KEY_COLS], in_=bk.unsqueeze(0))
+        nc.sync.dma_start(out=bias_row[0:1, KEY_COLS:COLS], in_=bv.unsqueeze(0))
         for g in range(X_BUFS):
             load(g)
 
         ident = consts.tile([P, P], F32)
         make_identity(nc, ident[:])
+        ident_bf = consts.tile([P, P], BF16)
+        make_identity(nc, ident_bf[:])
         gamma_bf = consts.tile([P, HEADS], BF16)
         nc.gpsimd.dma_start(
             out=gamma_bf[:], in_=gamma.rearrange("o h x y -> (o h x y)").partition_broadcast(P)
@@ -203,6 +224,16 @@ def tile_ufoattention_pa_t_kernel(tc, queries, Wk, bk, Wv, bv, gamma, out):
         nc.tensor.matmul(out=bias_bank[:], lhsT=ones[:], rhs=bias_row[:], start=True, stop=True)
         bias = consts.tile([P, COLS], F32)
         nc.scalar.copy(out=bias[:], in_=bias_bank[:])
+        last_bias_bank = proj_pool.tile([P, HEAD_DIM], F32, name="proj_bank")
+        nc.tensor.matmul(
+            out=last_bias_bank[:],
+            lhsT=bias_row[:, LAST_COLS],
+            rhs=ones[:, 0:HEAD_DIM],
+            start=True,
+            stop=True,
+        )
+        last_bias = consts.tile([P, 1], F32)
+        nc.scalar.copy(out=last_bias[:], in_=last_bias_bank[:, 0:1])
 
         w_grouped = consts.tile([P, COLS, PACK], BF16, align_bytes=64)
         nc.vector.tensor_copy(
@@ -223,15 +254,13 @@ def tile_ufoattention_pa_t_kernel(tc, queries, Wk, bk, Wv, bv, gamma, out):
 
         for i in range(-3, GROUPS):
             if 0 <= i + 1 < GROUPS:
-                project(i + 1, VECTOR_BLOCKS)
-                stage_last_block(i + 1)
+                project_last_block(i + 1)
+                add_bias_to_last_block(i + 1)
             for block in range(VECTOR_BLOCKS):
                 if i >= 0:
                     add_bias(i, block)
                 if 0 <= i + 1 < GROUPS:
                     project(i + 1, block)
-            if i >= 0:
-                add_bias_to_last_block(i)
             if 0 <= i + 2 < GROUPS:
                 quantise_x(i + 2)
             if i >= 0:
@@ -240,10 +269,10 @@ def tile_ufoattention_pa_t_kernel(tc, queries, Wk, bk, Wv, bv, gamma, out):
                 transpose(i + 3)
                 if i + 3 + X_BUFS < GROUPS:
                     load(i + 3 + X_BUFS)
-            if i >= 0:
-                accumulate(i)
-                if i % GROUPS_PER_BATCH == GROUPS_PER_BATCH - 1:
-                    collect(i // GROUPS_PER_BATCH)
+            if 0 <= i + 1 < GROUPS:
+                transpose_last_block(i + 1)
+            if i >= 0 and i % GROUPS_PER_BATCH == GROUPS_PER_BATCH - 1:
+                second_product(i // GROUPS_PER_BATCH)
 
         gamma_rows = consts.tile([P, HEAD_PAIRS], F32)
         for half in range(2):

@@ -40,6 +40,7 @@ def tile_ufoattention_pa_t_kernel(tc, queries, Wk, bk, Wv, bv, gamma, out):
         consts = ctx.enter_context(tc.tile_pool(name="consts", bufs=1))
         x_pool = ctx.enter_context(tc.tile_pool(name="x", bufs=X_BUFS))
         work = ctx.enter_context(tc.tile_pool(name="work", bufs=2))
+        x_grouped_pool = ctx.enter_context(tc.tile_pool(name="x_grouped", bufs=3))
         batch_pool = ctx.enter_context(tc.tile_pool(name="batch", bufs=2))
         xt_pool = ctx.enter_context(tc.psum_pool(name="xt", bufs=3))
         proj_pool = ctx.enter_context(tc.psum_pool(name="proj", bufs=VECTOR_BLOCKS))
@@ -66,7 +67,7 @@ def tile_ufoattention_pa_t_kernel(tc, queries, Wk, bk, Wv, bv, gamma, out):
 
         def transpose(g):
             x_words = x_tiles[g][:].bitcast(F32)
-            grouped = work.tile([P, GROUP * PACK], BF16, align_bytes=64, name="x_grouped")
+            grouped = x_grouped_pool.tile([P, GROUP * PACK], BF16, align_bytes=64, name="x_grouped")
             grouped_words = grouped[:].bitcast(F32)
             for bank in range(2):
                 xt = xt_pool.tile([P, 2, 2, P], F32, name="xt", tag="xt")
@@ -252,7 +253,7 @@ def tile_ufoattention_pa_t_kernel(tc, queries, Wk, bk, Wv, bv, gamma, out):
         squares = consts.tile([P, HEAD_DIM], F32)
         sum_squares = consts.tile([P, BATCHES * HEAD_PAIRS], F32)
 
-        for i in range(-3, GROUPS):
+        for i in range(-4, GROUPS):
             if 0 <= i + 1 < GROUPS:
                 project_last_block(i + 1)
                 add_bias_to_last_block(i + 1)
@@ -265,12 +266,12 @@ def tile_ufoattention_pa_t_kernel(tc, queries, Wk, bk, Wv, bv, gamma, out):
                 quantise_x(i + 2)
             if i >= 0:
                 quantise_kv(i)
-            if i + 3 < GROUPS:
-                transpose(i + 3)
-                if i + 3 + X_BUFS < GROUPS:
-                    load(i + 3 + X_BUFS)
             if 0 <= i + 1 < GROUPS:
                 transpose_last_block(i + 1)
+            if i + 4 < GROUPS:
+                transpose(i + 4)
+                if i + 4 + X_BUFS < GROUPS:
+                    load(i + 4 + X_BUFS)
             if i >= 0 and i % GROUPS_PER_BATCH == GROUPS_PER_BATCH - 1:
                 second_product(i // GROUPS_PER_BATCH)
 

@@ -40,7 +40,7 @@ def tile_ufoattention_pa_t_kernel(tc, queries, Wk, bk, Wv, bv, gamma, out):
         consts = ctx.enter_context(tc.tile_pool(name="consts", bufs=1))
         x_pool = ctx.enter_context(tc.tile_pool(name="x", bufs=X_BUFS))
         work = ctx.enter_context(tc.tile_pool(name="work", bufs=2))
-        x_grouped_pool = ctx.enter_context(tc.tile_pool(name="x_grouped", bufs=3))
+        kv_grouped_pool = ctx.enter_context(tc.tile_pool(name="kv_grouped", bufs=3))
         batch_pool = ctx.enter_context(tc.tile_pool(name="batch", bufs=2))
         xt_pool = ctx.enter_context(tc.psum_pool(name="xt", bufs=3))
         proj_pool = ctx.enter_context(tc.psum_pool(name="proj", bufs=VECTOR_BLOCKS))
@@ -67,7 +67,7 @@ def tile_ufoattention_pa_t_kernel(tc, queries, Wk, bk, Wv, bv, gamma, out):
 
         def transpose(g):
             x_words = x_tiles[g][:].bitcast(F32)
-            grouped = x_grouped_pool.tile([P, GROUP * PACK], BF16, align_bytes=64, name="x_grouped")
+            grouped = work.tile([P, GROUP * PACK], BF16, align_bytes=64, name="x_grouped")
             grouped_words = grouped[:].bitcast(F32)
             for bank in range(2):
                 xt = xt_pool.tile([P, 2, 2, P], F32, name="xt", tag="xt")
@@ -140,7 +140,9 @@ def tile_ufoattention_pa_t_kernel(tc, queries, Wk, bk, Wv, bv, gamma, out):
             )
 
         def transpose_last_block(g):
-            kv_grouped[g] = work.tile([P, COLS, PACK], BF16, align_bytes=64, name="kv_grouped")
+            kv_grouped[g] = kv_grouped_pool.tile(
+                [P, COLS, PACK], BF16, align_bytes=64, name="kv_grouped"
+            )
             back = xt_pool.tile([P, PACK, BLOCK], BF16, name="back", tag="xt")
             for t in range(PACK):
                 nc.tensor.transpose(
@@ -253,27 +255,27 @@ def tile_ufoattention_pa_t_kernel(tc, queries, Wk, bk, Wv, bv, gamma, out):
         squares = consts.tile([P, HEAD_DIM], F32)
         sum_squares = consts.tile([P, BATCHES * HEAD_PAIRS], F32)
 
-        for i in range(-4, GROUPS):
+        for i in range(-3, GROUPS + 1):
             if 0 <= i + 1 < GROUPS:
                 project_last_block(i + 1)
                 add_bias_to_last_block(i + 1)
             for block in range(VECTOR_BLOCKS):
-                if i >= 0:
+                if 0 <= i < GROUPS:
                     add_bias(i, block)
                 if 0 <= i + 1 < GROUPS:
                     project(i + 1, block)
+            if i >= 1:
+                quantise_kv(i - 1)
             if 0 <= i + 2 < GROUPS:
                 quantise_x(i + 2)
-            if i >= 0:
-                quantise_kv(i)
+            if i + 3 < GROUPS:
+                transpose(i + 3)
+                if i + 3 + X_BUFS < GROUPS:
+                    load(i + 3 + X_BUFS)
             if 0 <= i + 1 < GROUPS:
                 transpose_last_block(i + 1)
-            if i + 4 < GROUPS:
-                transpose(i + 4)
-                if i + 4 + X_BUFS < GROUPS:
-                    load(i + 4 + X_BUFS)
-            if i >= 0 and i % GROUPS_PER_BATCH == GROUPS_PER_BATCH - 1:
-                second_product(i // GROUPS_PER_BATCH)
+            if i >= 1 and i % GROUPS_PER_BATCH == 0:
+                second_product(i // GROUPS_PER_BATCH - 1)
 
         gamma_rows = consts.tile([P, HEAD_PAIRS], F32)
         for half in range(2):

@@ -23,13 +23,21 @@ KEY_COLS = HEADS * HEAD_DIM
 COLS = 2 * KEY_COLS
 BLOCK = P
 BLOCKS = COLS // BLOCK
-VECTOR_BLOCKS = BLOCKS - 1
-LAST_COLS = slice(VECTOR_BLOCKS * BLOCK, COLS)
+KEY_BLOCKS = KEY_COLS // BLOCK
+VALUE_BLOCKS = BLOCKS - KEY_BLOCKS
 HEAD_PAIRS = HEADS // 2
 WORDS = FEATURES // 2
 X_BUFS = 8
 
 FLOPS = 2 * BATCHES * TOKENS_PER_BATCH * (FEATURES * COLS + HEADS * HEAD_DIM * HEAD_DIM)
+
+
+def block_cols(block):
+    return slice(block * BLOCK, (block + 1) * BLOCK)
+
+
+def half_rows(half):
+    return slice(half * HEAD_DIM, (half + 1) * HEAD_DIM)
 
 
 def tile_ufoattention_pa_t_kernel(tc, queries, Wk, bk, Wv, bv, gamma, out):
@@ -39,23 +47,26 @@ def tile_ufoattention_pa_t_kernel(tc, queries, Wk, bk, Wv, bv, gamma, out):
     with ExitStack() as ctx:
         consts = ctx.enter_context(tc.tile_pool(name="consts", bufs=1))
         x_pool = ctx.enter_context(tc.tile_pool(name="x", bufs=X_BUFS))
-        work = ctx.enter_context(tc.tile_pool(name="work", bufs=2))
-        kv_grouped_pool = ctx.enter_context(tc.tile_pool(name="kv_grouped", bufs=3))
+        work = ctx.enter_context(tc.tile_pool(name="work", bufs=3))
         batch_pool = ctx.enter_context(tc.tile_pool(name="batch", bufs=2))
-        xt_pool = ctx.enter_context(tc.psum_pool(name="xt", bufs=3))
-        proj_pool = ctx.enter_context(tc.psum_pool(name="proj", bufs=VECTOR_BLOCKS))
-        last_pool = ctx.enter_context(tc.psum_pool(name="last", bufs=1))
+        xt_pool = ctx.enter_context(tc.psum_pool(name="xt", bufs=2))
+        key_pool = ctx.enter_context(tc.psum_pool(name="key", bufs=KEY_BLOCKS))
+        value_pool = ctx.enter_context(tc.psum_pool(name="value", bufs=VALUE_BLOCKS))
+        back_pool = ctx.enter_context(tc.psum_pool(name="back", bufs=1))
         kv_pool = ctx.enter_context(tc.psum_pool(name="kv", bufs=1))
         ctx.enter_context(tc.manual_schedule())
 
         x_tiles = {}
+        xt_banks = {}
         x_grouped = {}
         x_mx = {}
-        proj_banks = {}
-        last_banks = {}
-        last_rounded = {}
+        key_banks = {}
+        value_banks = {}
+        rounded = {}
+        back_banks = {}
         kv_grouped = {}
         kv_mx = {}
+        kv_sums = {}
 
         def load(g):
             x_sb = x_pool.tile([P, PACK * FEATURES], BF16)
@@ -67,21 +78,24 @@ def tile_ufoattention_pa_t_kernel(tc, queries, Wk, bk, Wv, bv, gamma, out):
 
         def transpose(g):
             x_words = x_tiles[g][:].bitcast(F32)
-            grouped = work.tile([P, GROUP * PACK], BF16, align_bytes=64, name="x_grouped")
-            grouped_words = grouped[:].bitcast(F32)
             for bank in range(2):
                 xt = xt_pool.tile([P, 2, 2, P], F32, name="xt", tag="xt")
                 for s in range(2):
                     for u in range(2):
                         first = ((2 * bank + s) * 2 + u) * P
                         nc.tensor.transpose(xt[:, s, u, :], x_words[:, first : first + P], ident[:])
-                nc.scalar.copy(
-                    out=grouped_words[:, bank * 4 * P : (bank + 1) * 4 * P].rearrange(
-                        "q (s p u) -> q s p u", s=2, u=2
-                    ),
-                    in_=xt[:].rearrange("q s u p -> q s p u"),
-                )
-            x_grouped[g] = grouped
+                xt_banks[(g, bank)] = xt
+
+        def copy_out(g, bank):
+            if bank == 0:
+                x_grouped[g] = work.tile([P, GROUP * PACK], BF16, align_bytes=64, name="x_grouped")
+            grouped_words = x_grouped[g][:].bitcast(F32)
+            nc.scalar.copy(
+                out=grouped_words[:, bank * 4 * P : (bank + 1) * 4 * P].rearrange(
+                    "q (s p u) -> q s p u", s=2, u=2
+                ),
+                in_=xt_banks[(g, bank)][:].rearrange("q s u p -> q s p u"),
+            )
 
         def quantise_x(g):
             words = work.tile([P, GROUP], U32, align_bytes=64, name="x_words")
@@ -89,10 +103,10 @@ def tile_ufoattention_pa_t_kernel(tc, queries, Wk, bk, Wv, bv, gamma, out):
             nc.vector.quantize_mx(out=words[:].bitcast(FP8X4), scales=scales[:], in_=x_grouped[g][:])
             x_mx[g] = (words, scales)
 
-        def project(g, block):
+        def project_keys(g, block):
             words, scales = x_mx[g]
-            cols = slice(block * BLOCK, (block + 1) * BLOCK)
-            bank = proj_pool.tile([P, PACK, BLOCK], F32, name="proj_bank")
+            cols = block_cols(block)
+            bank = key_pool.tile([P, PACK, BLOCK], F32, name="key_bank")
             for t in range(PACK):
                 slot = slice(t * P, (t + 1) * P)
                 nc.tensor.matmul_mx(
@@ -104,52 +118,63 @@ def tile_ufoattention_pa_t_kernel(tc, queries, Wk, bk, Wv, bv, gamma, out):
                     start=True,
                     stop=True,
                 )
-            proj_banks[(g, block)] = bank
+            key_banks[(g, block)] = bank
 
-        def add_bias(g, block):
-            cols = slice(block * BLOCK, (block + 1) * BLOCK)
-            nc.vector.tensor_tensor(
-                out=kv_grouped[g][:, cols, :],
-                in0=proj_banks[(g, block)][:].rearrange("p t c -> p c t"),
-                in1=bias[:, cols].unsqueeze(2).to_broadcast([P, BLOCK, PACK]),
-                op=ADD,
-            )
-
-        def project_last_block(g):
+        def project_values(g, block):
             words, scales = x_mx[g]
-            bank = last_pool.tile([P, GROUP], F32, name="last_bank")
+            cols = block_cols(KEY_BLOCKS + block)
+            bank = value_pool.tile([P, GROUP], F32, name="value_bank")
             nc.tensor.matmul_mx(
                 out=bank[:],
-                lhsT=w_words[:, LAST_COLS].bitcast(FP8X4),
-                lhsT_scale=w_scales[:, LAST_COLS],
+                lhsT=w_words[:, cols].bitcast(FP8X4),
+                lhsT_scale=w_scales[:, cols],
                 rhs=words[:].bitcast(FP8X4),
                 rhs_scale=scales[:],
                 start=True,
                 stop=True,
             )
-            last_banks[g] = bank
+            value_banks[(g, block)] = bank
 
-        def add_bias_to_last_block(g):
-            last_rounded[g] = work.tile([P, GROUP], BF16, name="last_rounded")
+        def add_key_bias(g, block):
+            if block == 0:
+                kv_grouped[g] = work.tile([P, COLS * PACK], BF16, align_bytes=64, name="kv_grouped")
+            first = block * BLOCK * PACK
+            nc.vector.tensor_tensor(
+                out=kv_grouped[g][:, first : first + BLOCK * PACK].rearrange(
+                    "p (c t) -> p c t", t=PACK
+                ),
+                in0=key_banks[(g, block)][:].rearrange("p t c -> p c t"),
+                in1=key_bias[:, block_cols(block)].unsqueeze(2).to_broadcast([P, BLOCK, PACK]),
+                op=ADD,
+            )
+
+        def add_value_bias(g, block):
+            rounded[(g, block)] = work.tile([P, GROUP], BF16, name="rounded" + str(block))
             nc.scalar.activation(
-                out=last_rounded[g][:],
-                in_=last_banks[g][:],
+                out=rounded[(g, block)][:].rearrange("c (u p e) -> c u p e", u=2, e=2),
+                in_=value_banks[(g, block)][:].rearrange("c (u e p) -> c u p e", u=2, e=2),
                 func=ACT.Identity,
-                bias=last_bias[:, 0:1],
+                bias=value_bias[:, block : block + 1],
                 scale=1.0,
             )
 
-        def transpose_last_block(g):
-            kv_grouped[g] = kv_grouped_pool.tile(
-                [P, COLS, PACK], BF16, align_bytes=64, name="kv_grouped"
-            )
-            back = xt_pool.tile([P, PACK, BLOCK], BF16, name="back", tag="xt")
-            for t in range(PACK):
-                nc.tensor.transpose(
-                    back[:, t, :], last_rounded[g][:, t * P : (t + 1) * P], ident_bf[:]
-                )
-            nc.scalar.copy(
-                out=kv_grouped[g][:, LAST_COLS, :], in_=back[:].rearrange("p t c -> p c t")
+        def transpose_back(g):
+            back = back_pool.tile([P, VALUE_BLOCKS, 2, BLOCK], F32, name="back")
+            for block in range(VALUE_BLOCKS):
+                pairs = rounded[(g, block)][:].bitcast(F32)
+                for u in range(2):
+                    nc.tensor.transpose(
+                        back[:, block, u, :], pairs[:, u * P : (u + 1) * P], ident[:]
+                    )
+            back_banks[g] = back
+
+        def copy_back(g, block, copy):
+            first = (KEY_BLOCKS + block) * BLOCK * 2
+            copy(
+                out=kv_grouped[g][:]
+                .bitcast(F32)[:, first : first + BLOCK * 2]
+                .rearrange("p (c u) -> p c u", u=2),
+                in_=back_banks[g][:, block, :, :].rearrange("p u c -> p c u"),
             )
 
         def quantise_kv(g):
@@ -163,36 +188,22 @@ def tile_ufoattention_pa_t_kernel(tc, queries, Wk, bk, Wv, bv, gamma, out):
             nc.vector.quantize_mx(
                 out=words[:, step, :].bitcast(FP8X4),
                 scales=scales[:, step, :],
-                in_=kv_grouped[g][:].rearrange("p c t -> p (c t)"),
+                in_=kv_grouped[g][:],
             )
 
-        def second_product(b):
+        def second_product(b, pair, step):
             words, scales = kv_mx[b]
-            kv_sums = kv_pool.tile([P, HEAD_PAIRS, BLOCK], F32)
-            for pair in range(HEAD_PAIRS):
-                k_cols = slice(pair * BLOCK, (pair + 1) * BLOCK)
-                v_cols = slice(KEY_COLS + pair * BLOCK, KEY_COLS + (pair + 1) * BLOCK)
-                for step in range(GROUPS_PER_BATCH):
-                    nc.tensor.matmul_mx(
-                        out=kv_sums[:, pair, :],
-                        lhsT=words[:, step, k_cols].bitcast(FP8X4),
-                        lhsT_scale=scales[:, step, k_cols],
-                        rhs=words[:, step, v_cols].bitcast(FP8X4),
-                        rhs_scale=scales[:, step, v_cols],
-                        start=(step == 0),
-                        stop=(step == GROUPS_PER_BATCH - 1),
-                    )
-            for pair in range(HEAD_PAIRS):
-                place = b * HEAD_PAIRS + pair
-                for half in range(2):
-                    rows = slice(half * HEAD_DIM, (half + 1) * HEAD_DIM)
-                    nc.scalar.copy(out=kv_all[rows, place, :], in_=kv_sums[rows, pair, rows])
-                nc.scalar.activation(
-                    out=squares[:],
-                    in_=kv_all[:, place, :],
-                    func=ACT.Square,
-                    accum_out=sum_squares[:, place : place + 1],
-                )
+            k_cols = block_cols(pair)
+            v_cols = block_cols(KEY_BLOCKS + pair)
+            nc.tensor.matmul_mx(
+                out=kv_sums[(b, pair)][:],
+                lhsT=words[:, step, k_cols].bitcast(FP8X4),
+                lhsT_scale=scales[:, step, k_cols],
+                rhs=words[:, step, v_cols].bitcast(FP8X4),
+                rhs_scale=scales[:, step, v_cols],
+                start=(step == 0),
+                stop=(step == GROUPS_PER_BATCH - 1),
+            )
 
         w_raw = consts.tile([P, 2, PACK, KEY_COLS], BF16)
         for which, w in enumerate((Wk, Wv)):
@@ -209,8 +220,6 @@ def tile_ufoattention_pa_t_kernel(tc, queries, Wk, bk, Wv, bv, gamma, out):
 
         ident = consts.tile([P, P], F32)
         make_identity(nc, ident[:])
-        ident_bf = consts.tile([P, P], BF16)
-        make_identity(nc, ident_bf[:])
         gamma_bf = consts.tile([P, HEADS], BF16)
         nc.gpsimd.dma_start(
             out=gamma_bf[:], in_=gamma.rearrange("o h x y -> (o h x y)").partition_broadcast(P)
@@ -223,20 +232,23 @@ def tile_ufoattention_pa_t_kernel(tc, queries, Wk, bk, Wv, bv, gamma, out):
 
         ones = consts.tile([P, P], BF16)
         nc.vector.memset(ones[:], 1.0)
-        bias_bank = proj_pool.tile([P, COLS], F32, name="proj_bank")
-        nc.tensor.matmul(out=bias_bank[:], lhsT=ones[:], rhs=bias_row[:], start=True, stop=True)
-        bias = consts.tile([P, COLS], F32)
-        nc.scalar.copy(out=bias[:], in_=bias_bank[:])
-        last_bias_bank = proj_pool.tile([P, HEAD_DIM], F32, name="proj_bank")
+        key_bias_bank = key_pool.tile([P, KEY_COLS], F32, name="key_bank")
         nc.tensor.matmul(
-            out=last_bias_bank[:],
-            lhsT=bias_row[:, LAST_COLS],
-            rhs=ones[:, 0:HEAD_DIM],
-            start=True,
-            stop=True,
+            out=key_bias_bank[:], lhsT=ones[:], rhs=bias_row[:, 0:KEY_COLS], start=True, stop=True
         )
-        last_bias = consts.tile([P, 1], F32)
-        nc.scalar.copy(out=last_bias[:], in_=last_bias_bank[:, 0:1])
+        key_bias = consts.tile([P, KEY_COLS], F32)
+        nc.scalar.copy(out=key_bias[:], in_=key_bias_bank[:])
+        value_bias_bank = key_pool.tile([P, VALUE_BLOCKS, HEAD_DIM], F32, name="key_bank")
+        for block in range(VALUE_BLOCKS):
+            nc.tensor.matmul(
+                out=value_bias_bank[:, block, :],
+                lhsT=bias_row[:, block_cols(KEY_BLOCKS + block)],
+                rhs=ones[:, 0:HEAD_DIM],
+                start=True,
+                stop=True,
+            )
+        value_bias = consts.tile([P, VALUE_BLOCKS], F32)
+        nc.scalar.copy(out=value_bias[:], in_=value_bias_bank[:, :, 0])
 
         w_grouped = consts.tile([P, COLS, PACK], BF16, align_bytes=64)
         nc.vector.tensor_copy(
@@ -251,61 +263,131 @@ def tile_ufoattention_pa_t_kernel(tc, queries, Wk, bk, Wv, bv, gamma, out):
             in_=w_grouped[:].rearrange("q c t -> q (c t)"),
         )
 
-        kv_all = consts.tile([P, BATCHES * HEAD_PAIRS, HEAD_DIM], F32)
-        squares = consts.tile([P, HEAD_DIM], F32)
-        sum_squares = consts.tile([P, BATCHES * HEAD_PAIRS], F32)
+        gamma_rows = consts.tile([P, HEAD_PAIRS], F32)
+        for half in range(2):
+            nc.vector.tensor_copy(
+                out=gamma_rows[half_rows(half), :],
+                in_=gamma_bf[half_rows(half), :].rearrange("p (pair half) -> p half pair", half=2)[
+                    :, half, :
+                ],
+            )
 
+        last_batch = BATCHES - 1
+        places = last_batch * HEAD_PAIRS
+        kv_all = consts.tile([P, places, BLOCK], F32)
+        squares = consts.tile([P, HEAD_DIM], F32)
+        sum_squares = consts.tile([P, places], F32)
+        norms = consts.tile([P, last_batch, HEAD_PAIRS], F32)
+        last_sum_squares = consts.tile([P, HEAD_PAIRS], F32)
+
+        def add_squares(product, accumulator):
+            for half in range(2):
+                rows = half_rows(half)
+                nc.scalar.activation(
+                    out=squares[rows, :],
+                    in_=product[rows, rows],
+                    func=ACT.Square,
+                    accum_out=accumulator[rows, :],
+                )
+
+        drain_turn = GROUPS - 3
         for i in range(-3, GROUPS + 1):
-            if 0 <= i + 1 < GROUPS:
-                project_last_block(i + 1)
-                add_bias_to_last_block(i + 1)
-            for block in range(VECTOR_BLOCKS):
-                if 0 <= i < GROUPS:
-                    add_bias(i, block)
-                if 0 <= i + 1 < GROUPS:
-                    project(i + 1, block)
-            if i >= 1:
-                quantise_kv(i - 1)
-            if 0 <= i + 2 < GROUPS:
-                quantise_x(i + 2)
             if i + 3 < GROUPS:
                 transpose(i + 3)
                 if i + 3 + X_BUFS < GROUPS:
                     load(i + 3 + X_BUFS)
+            if 0 <= i < GROUPS:
+                for block in range(KEY_BLOCKS):
+                    add_key_bias(i, block)
+                transpose_back(i)
+            if i + 3 < GROUPS:
+                copy_out(i + 3, 0)
+            if 0 <= i < GROUPS:
+                copy_back(i, 0, nc.scalar.copy)
+            if i + 3 < GROUPS:
+                copy_out(i + 3, 1)
             if 0 <= i + 1 < GROUPS:
-                transpose_last_block(i + 1)
-            if i >= 1 and i % GROUPS_PER_BATCH == 0:
-                second_product(i // GROUPS_PER_BATCH - 1)
+                for block in range(VALUE_BLOCKS):
+                    project_values(i + 1, block)
+                for block in range(KEY_BLOCKS):
+                    project_keys(i + 1, block)
+                for block in range(VALUE_BLOCKS):
+                    add_value_bias(i + 1, block)
+            if i >= 1:
+                quantise_kv(i - 1)
+            if 0 <= i < GROUPS:
+                copy_back(i, 1, nc.vector.tensor_copy)
+            if 0 <= i + 2 < GROUPS:
+                quantise_x(i + 2)
+            b, turn = divmod(i - GROUPS_PER_BATCH + 2, GROUPS_PER_BATCH)
+            if 0 <= b < last_batch:
+                pair, part = divmod(turn, GROUPS_PER_BATCH // HEAD_PAIRS)
+                if part == 0:
+                    kv_sums[(b, pair)] = kv_pool.tile([P, BLOCK], F32, name="kv_bank")
+                for step in (2 * part, 2 * part + 1):
+                    second_product(b, pair, step)
+                if part == GROUPS_PER_BATCH // HEAD_PAIRS - 1:
+                    nc.scalar.copy(out=kv_all[:, b * HEAD_PAIRS + pair, :], in_=kv_sums[(b, pair)][:])
+            if i == drain_turn:
+                for pair in range(HEAD_PAIRS):
+                    kv_sums[(last_batch, pair)] = xt_pool.tile([P, BLOCK], F32, name="last_bank", tag="xt")
+            if i >= drain_turn:
+                first_step = 0 if i == drain_turn else i - 2 - last_batch * GROUPS_PER_BATCH
+                end_step = GROUPS_PER_BATCH if i == GROUPS else i - 1 - last_batch * GROUPS_PER_BATCH
+                for pair in range(HEAD_PAIRS):
+                    for step in range(first_step, end_step):
+                        second_product(last_batch, pair, step)
+            if i == GROUPS - 1:
+                for place in range(places):
+                    add_squares(kv_all[:, place, :], sum_squares[:, place : place + 1])
+                nc.scalar.activation(
+                    out=norms[:].rearrange("p b pair -> p (b pair)"), in_=sum_squares[:], func=ACT.Sqrt
+                )
 
-        gamma_rows = consts.tile([P, HEAD_PAIRS], F32)
-        for half in range(2):
-            rows = slice(half * HEAD_DIM, (half + 1) * HEAD_DIM)
-            nc.vector.tensor_copy(
-                out=gamma_rows[rows, :],
-                in_=gamma_bf[rows, :].rearrange("p (pair half) -> p half pair", half=2)[:, half, :],
-            )
-        norms = consts.tile([P, BATCHES, HEAD_PAIRS], F32)
-        nc.scalar.activation(
-            out=norms[:].rearrange("p b pair -> p (b pair)"), in_=sum_squares[:], func=ACT.Sqrt
-        )
-        gains = consts.tile([P, BATCHES, HEAD_PAIRS], F32)
+        gains = consts.tile([P, last_batch, HEAD_PAIRS], F32)
         nc.vector.reciprocal(out=gains[:], in_=norms[:])
         nc.vector.tensor_tensor(
             out=gains[:],
             in0=gains[:],
-            in1=gamma_rows[:].unsqueeze(1).to_broadcast([P, BATCHES, HEAD_PAIRS]),
+            in1=gamma_rows[:].unsqueeze(1).to_broadcast([P, last_batch, HEAD_PAIRS]),
             op=MULT,
         )
-        result = consts.tile([P, BATCHES * HEAD_PAIRS, HEAD_DIM], F32)
-        nc.vector.tensor_tensor(
-            out=result[:],
-            in0=kv_all[:],
-            in1=gains[:]
-            .rearrange("p b pair -> p (b pair)")
-            .unsqueeze(2)
-            .to_broadcast([P, BATCHES * HEAD_PAIRS, HEAD_DIM]),
-            op=MULT,
-        )
+        result = consts.tile([P, places, HEAD_DIM], F32)
+        for half in range(2):
+            rows = half_rows(half)
+            nc.vector.tensor_tensor(
+                out=result[rows, :, :],
+                in0=kv_all[rows, :, rows],
+                in1=gains[rows, :, :]
+                .rearrange("p b pair -> p (b pair)")
+                .unsqueeze(2)
+                .to_broadcast([HEAD_DIM, places, HEAD_DIM]),
+                op=MULT,
+            )
         nc.sync.dma_start(
-            out=out.rearrange("b (pair half) i j -> (half i) (b pair) j", half=2), in_=result[:]
+            out=out[0:last_batch].rearrange("b (pair half) i j -> (half i) (b pair) j", half=2),
+            in_=result[:],
+        )
+
+        for pair in range(HEAD_PAIRS):
+            add_squares(kv_sums[(last_batch, pair)], last_sum_squares[:, pair : pair + 1])
+        last_norms = consts.tile([P, HEAD_PAIRS], F32)
+        nc.scalar.activation(out=last_norms[:], in_=last_sum_squares[:], func=ACT.Sqrt)
+        last_gains = consts.tile([P, HEAD_PAIRS], F32)
+        nc.vector.reciprocal(out=last_gains[:], in_=last_norms[:])
+        last_result = consts.tile([P, HEAD_PAIRS, HEAD_DIM], F32)
+        for pair in range(HEAD_PAIRS):
+            for half in range(2):
+                rows = half_rows(half)
+                nc.vector.tensor_scalar(
+                    out=last_result[rows, pair, :],
+                    in0=kv_sums[(last_batch, pair)][rows, rows],
+                    scalar1=last_gains[rows, pair : pair + 1],
+                    scalar2=gamma_rows[rows, pair : pair + 1],
+                    op0=MULT,
+                    op1=MULT,
+                )
+        nc.sync.dma_start(
+            out=out[last_batch].rearrange("(pair half) i j -> (half i) pair j", half=2),
+            in_=last_result[:],
         )

@@ -47,12 +47,9 @@ def tile_ufoattention_pa_t_kernel(tc, queries, Wk, bk, Wv, bv, gamma, out):
     with ExitStack() as ctx:
         consts = ctx.enter_context(tc.tile_pool(name="consts", bufs=1))
         x_pool = ctx.enter_context(tc.tile_pool(name="x", bufs=X_BUFS))
-        work = ctx.enter_context(tc.tile_pool(name="work", bufs=3))
+        work = ctx.enter_context(tc.tile_pool(name="work", bufs=4))
         batch_pool = ctx.enter_context(tc.tile_pool(name="batch", bufs=2))
-        xt_pool = ctx.enter_context(tc.psum_pool(name="xt", bufs=2))
-        key_pool = ctx.enter_context(tc.psum_pool(name="key", bufs=KEY_BLOCKS))
-        value_pool = ctx.enter_context(tc.psum_pool(name="value", bufs=VALUE_BLOCKS))
-        back_pool = ctx.enter_context(tc.psum_pool(name="back", bufs=1))
+        ring = ctx.enter_context(tc.psum_pool(name="ring", bufs=7))
         kv_pool = ctx.enter_context(tc.psum_pool(name="kv", bufs=1))
         ctx.enter_context(tc.manual_schedule())
 
@@ -79,7 +76,7 @@ def tile_ufoattention_pa_t_kernel(tc, queries, Wk, bk, Wv, bv, gamma, out):
         def transpose(g):
             x_words = x_tiles[g][:].bitcast(F32)
             for bank in range(2):
-                xt = xt_pool.tile([P, 2, 2, P], F32, name="xt", tag="xt")
+                xt = ring.tile([P, 2, 2, P], F32, name="xt", tag="ring")
                 for s in range(2):
                     for u in range(2):
                         first = ((2 * bank + s) * 2 + u) * P
@@ -106,7 +103,7 @@ def tile_ufoattention_pa_t_kernel(tc, queries, Wk, bk, Wv, bv, gamma, out):
         def project_keys(g, block):
             words, scales = x_mx[g]
             cols = block_cols(block)
-            bank = key_pool.tile([P, PACK, BLOCK], F32, name="key_bank")
+            bank = ring.tile([P, PACK, BLOCK], F32, name="key_bank", tag="ring")
             for t in range(PACK):
                 slot = slice(t * P, (t + 1) * P)
                 nc.tensor.matmul_mx(
@@ -123,7 +120,7 @@ def tile_ufoattention_pa_t_kernel(tc, queries, Wk, bk, Wv, bv, gamma, out):
         def project_values(g, block):
             words, scales = x_mx[g]
             cols = block_cols(KEY_BLOCKS + block)
-            bank = value_pool.tile([P, GROUP], F32, name="value_bank")
+            bank = ring.tile([P, GROUP], F32, name="value_bank", tag="ring")
             nc.tensor.matmul_mx(
                 out=bank[:],
                 lhsT=w_words[:, cols].bitcast(FP8X4),
@@ -159,7 +156,7 @@ def tile_ufoattention_pa_t_kernel(tc, queries, Wk, bk, Wv, bv, gamma, out):
             )
 
         def transpose_back(g):
-            back = back_pool.tile([P, VALUE_BLOCKS, 2, BLOCK], F32, name="back")
+            back = ring.tile([P, VALUE_BLOCKS, 2, BLOCK], F32, name="back", tag="ring")
             for block in range(VALUE_BLOCKS):
                 pairs = rounded[(g, block)][:].bitcast(F32)
                 for u in range(2):
@@ -232,13 +229,13 @@ def tile_ufoattention_pa_t_kernel(tc, queries, Wk, bk, Wv, bv, gamma, out):
 
         ones = consts.tile([P, P], BF16)
         nc.vector.memset(ones[:], 1.0)
-        key_bias_bank = key_pool.tile([P, KEY_COLS], F32, name="key_bank")
+        key_bias_bank = ring.tile([P, KEY_COLS], F32, name="key_bias_bank", tag="ring")
         nc.tensor.matmul(
             out=key_bias_bank[:], lhsT=ones[:], rhs=bias_row[:, 0:KEY_COLS], start=True, stop=True
         )
         key_bias = consts.tile([P, KEY_COLS], F32)
         nc.scalar.copy(out=key_bias[:], in_=key_bias_bank[:])
-        value_bias_bank = key_pool.tile([P, VALUE_BLOCKS, HEAD_DIM], F32, name="key_bank")
+        value_bias_bank = ring.tile([P, VALUE_BLOCKS, HEAD_DIM], F32, name="value_bias_bank", tag="ring")
         for block in range(VALUE_BLOCKS):
             nc.tensor.matmul(
                 out=value_bias_bank[:, block, :],
@@ -263,15 +260,6 @@ def tile_ufoattention_pa_t_kernel(tc, queries, Wk, bk, Wv, bv, gamma, out):
             in_=w_grouped[:].rearrange("q c t -> q (c t)"),
         )
 
-        gamma_rows = consts.tile([P, HEAD_PAIRS], F32)
-        for half in range(2):
-            nc.vector.tensor_copy(
-                out=gamma_rows[half_rows(half), :],
-                in_=gamma_bf[half_rows(half), :].rearrange("p (pair half) -> p half pair", half=2)[
-                    :, half, :
-                ],
-            )
-
         last_batch = BATCHES - 1
         places = last_batch * HEAD_PAIRS
         kv_all = consts.tile([P, places, BLOCK], F32)
@@ -290,84 +278,113 @@ def tile_ufoattention_pa_t_kernel(tc, queries, Wk, bk, Wv, bv, gamma, out):
                     accum_out=accumulator[rows, :],
                 )
 
-        drain_turn = GROUPS - 3
-        for i in range(-3, GROUPS + 1):
-            if i + 3 < GROUPS:
-                transpose(i + 3)
-                if i + 3 + X_BUFS < GROUPS:
-                    load(i + 3 + X_BUFS)
-            if 0 <= i < GROUPS:
-                for block in range(KEY_BLOCKS):
-                    add_key_bias(i, block)
-                transpose_back(i)
-            if i + 3 < GROUPS:
-                copy_out(i + 3, 0)
-            if 0 <= i < GROUPS:
-                copy_back(i, 0, nc.scalar.copy)
-            if i + 3 < GROUPS:
-                copy_out(i + 3, 1)
-            if 0 <= i + 1 < GROUPS:
-                for block in range(VALUE_BLOCKS):
-                    project_values(i + 1, block)
-                for block in range(KEY_BLOCKS):
-                    project_keys(i + 1, block)
-                for block in range(VALUE_BLOCKS):
-                    add_value_bias(i + 1, block)
-            if i >= 1:
-                quantise_kv(i - 1)
-            if 0 <= i < GROUPS:
-                copy_back(i, 1, nc.vector.tensor_copy)
-            if 0 <= i + 2 < GROUPS:
-                quantise_x(i + 2)
-            b, turn = divmod(i - GROUPS_PER_BATCH + 2, GROUPS_PER_BATCH)
-            if 0 <= b < last_batch:
-                pair, part = divmod(turn, GROUPS_PER_BATCH // HEAD_PAIRS)
-                if part == 0:
-                    kv_sums[(b, pair)] = kv_pool.tile([P, BLOCK], F32, name="kv_bank")
-                for step in (2 * part, 2 * part + 1):
-                    second_product(b, pair, step)
-                if part == GROUPS_PER_BATCH // HEAD_PAIRS - 1:
-                    nc.scalar.copy(out=kv_all[:, b * HEAD_PAIRS + pair, :], in_=kv_sums[(b, pair)][:])
-            if i == drain_turn:
-                for pair in range(HEAD_PAIRS):
-                    kv_sums[(last_batch, pair)] = xt_pool.tile([P, BLOCK], F32, name="last_bank", tag="xt")
-            if i >= drain_turn:
-                first_step = 0 if i == drain_turn else i - 2 - last_batch * GROUPS_PER_BATCH
-                end_step = GROUPS_PER_BATCH if i == GROUPS else i - 1 - last_batch * GROUPS_PER_BATCH
-                for pair in range(HEAD_PAIRS):
-                    for step in range(first_step, end_step):
-                        second_product(last_batch, pair, step)
-            if i == GROUPS - 1:
-                for place in range(places):
-                    add_squares(kv_all[:, place, :], sum_squares[:, place : place + 1])
-                nc.scalar.activation(
-                    out=norms[:].rearrange("p b pair -> p (b pair)"), in_=sum_squares[:], func=ACT.Sqrt
-                )
+        def norms_of_first_batches():
+            for place in range(places):
+                add_squares(kv_all[:, place, :], sum_squares[:, place : place + 1])
+            nc.scalar.activation(
+                out=norms[:].rearrange("p b pair -> p (b pair)"), in_=sum_squares[:], func=ACT.Sqrt
+            )
 
-        gains = consts.tile([P, last_batch, HEAD_PAIRS], F32)
-        nc.vector.reciprocal(out=gains[:], in_=norms[:])
-        nc.vector.tensor_tensor(
-            out=gains[:],
-            in0=gains[:],
-            in1=gamma_rows[:].unsqueeze(1).to_broadcast([P, last_batch, HEAD_PAIRS]),
-            op=MULT,
-        )
-        result = consts.tile([P, places, HEAD_DIM], F32)
-        for half in range(2):
-            rows = half_rows(half)
+        gamma_rows = consts.tile([P, HEAD_PAIRS], F32)
+
+        def finish_first_batches():
+            for half in range(2):
+                nc.vector.tensor_copy(
+                    out=gamma_rows[half_rows(half), :],
+                    in_=gamma_bf[half_rows(half), :].rearrange("p (pair half) -> p half pair", half=2)[
+                        :, half, :
+                    ],
+                )
+            gains = consts.tile([P, last_batch, HEAD_PAIRS], F32)
+            nc.vector.reciprocal(out=gains[:], in_=norms[:])
             nc.vector.tensor_tensor(
-                out=result[rows, :, :],
-                in0=kv_all[rows, :, rows],
-                in1=gains[rows, :, :]
-                .rearrange("p b pair -> p (b pair)")
-                .unsqueeze(2)
-                .to_broadcast([HEAD_DIM, places, HEAD_DIM]),
+                out=gains[:],
+                in0=gains[:],
+                in1=gamma_rows[:].unsqueeze(1).to_broadcast([P, last_batch, HEAD_PAIRS]),
                 op=MULT,
             )
-        nc.sync.dma_start(
-            out=out[0:last_batch].rearrange("b (pair half) i j -> (half i) (b pair) j", half=2),
-            in_=result[:],
+            result = consts.tile([P, places, HEAD_DIM], F32)
+            for half in range(2):
+                rows = half_rows(half)
+                nc.vector.tensor_tensor(
+                    out=result[rows, :, :],
+                    in0=kv_all[rows, :, rows],
+                    in1=gains[rows, :, :]
+                    .rearrange("p b pair -> p (b pair)")
+                    .unsqueeze(2)
+                    .to_broadcast([HEAD_DIM, places, HEAD_DIM]),
+                    op=MULT,
+                )
+            nc.sync.dma_start(
+                out=out[0:last_batch].rearrange("b (pair half) i j -> (half i) (b pair) j", half=2),
+                in_=result[:],
+            )
+
+        turns = (
+            [[0], [1]] + [[g, g + 1] for g in range(2, GROUPS - 2, 2)] + [[GROUPS - 2], [GROUPS - 1]]
         )
+
+        def groups_of(n):
+            return turns[n] if 0 <= n < len(turns) else []
+
+        quantised = {}
+        passes = []
+        for b in range(BATCHES):
+            if b < last_batch:
+                passes += [(b, pair, s) for pair in range(HEAD_PAIRS) for s in range(GROUPS_PER_BATCH)]
+            else:
+                passes += [(b, pair, s) for s in range(GROUPS_PER_BATCH) for pair in range(HEAD_PAIRS)]
+
+        def second_products(n, limit):
+            while passes and limit > 0:
+                b, pair, step = passes[0]
+                group = b * GROUPS_PER_BATCH + step
+                if group not in quantised or quantised[group] >= n:
+                    break
+                if b == last_batch and n <= len(turns):
+                    break
+                passes.remove(passes[0])
+                limit -= 1
+                if step == 0:
+                    if b == last_batch:
+                        kv_sums[(b, pair)] = ring.tile([P, BLOCK], F32, name="last_bank", tag="ring")
+                    else:
+                        kv_sums[(b, pair)] = kv_pool.tile([P, BLOCK], F32, name="kv_bank")
+                second_product(b, pair, step)
+                if step == GROUPS_PER_BATCH - 1 and b < last_batch:
+                    nc.scalar.copy(out=kv_all[:, b * HEAD_PAIRS + pair, :], in_=kv_sums[(b, pair)][:])
+
+        for n in range(len(turns) + 3):
+            for g in groups_of(n - 1):
+                quantise_x(g)
+            for g in groups_of(n - 2):
+                for block in range(VALUE_BLOCKS):
+                    project_values(g, block)
+                    add_value_bias(g, block)
+            for g in groups_of(n - 2):
+                for block in range(KEY_BLOCKS):
+                    project_keys(g, block)
+                    add_key_bias(g, block)
+            second_products(n, 2 * len(groups_of(n)) if n < len(turns) else len(passes))
+            if n == len(turns) + 1:
+                finish_first_batches()
+            for g in groups_of(n):
+                transpose(g)
+                if g + X_BUFS < GROUPS:
+                    load(g + X_BUFS)
+                copy_out(g, 0)
+                copy_out(g, 1)
+            for g in groups_of(n - 2):
+                transpose_back(g)
+            for g in groups_of(n - 3):
+                quantise_kv(g)
+                quantised[g] = n
+            for g in groups_of(n - 2):
+                copy_back(g, 0, nc.scalar.copy)
+                copy_back(g, 1, nc.vector.tensor_copy)
+            if n == len(turns):
+                norms_of_first_batches()
+        second_products(len(turns) + 3, len(passes))
 
         for pair in range(HEAD_PAIRS):
             add_squares(kv_sums[(last_batch, pair)], last_sum_squares[:, pair : pair + 1])

@@ -27,6 +27,8 @@ KEY_BLOCKS = KEY_COLS // BLOCK
 VALUE_BLOCKS = BLOCKS - KEY_BLOCKS
 HEAD_PAIRS = HEADS // 2
 WORDS = FEATURES // 2
+HEAD_TURNS = 2
+TURN = 2
 X_BUFS = 8
 
 FLOPS = 2 * BATCHES * TOKENS_PER_BATCH * (FEATURES * COLS + HEADS * HEAD_DIM * HEAD_DIM)
@@ -47,7 +49,7 @@ def tile_ufoattention_pa_t_kernel(tc, queries, Wk, bk, Wv, bv, gamma, out):
     with ExitStack() as ctx:
         consts = ctx.enter_context(tc.tile_pool(name="consts", bufs=1))
         x_pool = ctx.enter_context(tc.tile_pool(name="x", bufs=X_BUFS))
-        work = ctx.enter_context(tc.tile_pool(name="work", bufs=4))
+        work = ctx.enter_context(tc.tile_pool(name="work", bufs=3))
         batch_pool = ctx.enter_context(tc.tile_pool(name="batch", bufs=2))
         ring = ctx.enter_context(tc.psum_pool(name="ring", bufs=7))
         kv_pool = ctx.enter_context(tc.psum_pool(name="kv", bufs=1))
@@ -60,17 +62,21 @@ def tile_ufoattention_pa_t_kernel(tc, queries, Wk, bk, Wv, bv, gamma, out):
         key_banks = {}
         value_banks = {}
         rounded = {}
-        back_banks = {}
         kv_grouped = {}
         kv_mx = {}
         kv_sums = {}
 
         def load(g):
             x_sb = x_pool.tile([P, PACK * FEATURES], BF16)
-            nc.sync.dma_start(
-                out=x_sb[:],
-                in_=tokens[g * GROUP : (g + 1) * GROUP, :].rearrange("(p t) d -> p (t d)", t=PACK),
-            )
+            pieces = 2 if g == 0 else 1
+            for piece in range(pieces):
+                part = slice(piece * PACK // pieces * FEATURES, (piece + 1) * PACK // pieces * FEATURES)
+                nc.sync.dma_start(
+                    out=x_sb[:, part],
+                    in_=tokens[g * GROUP : (g + 1) * GROUP, :].rearrange("(p t) d -> p (t d)", t=PACK)[
+                        :, part
+                    ],
+                )
             x_tiles[g] = x_sb
 
         def transpose(g):
@@ -83,22 +89,33 @@ def tile_ufoattention_pa_t_kernel(tc, queries, Wk, bk, Wv, bv, gamma, out):
                         nc.tensor.transpose(xt[:, s, u, :], x_words[:, first : first + P], ident[:])
                 xt_banks[(g, bank)] = xt
 
-        def copy_out(g, bank):
-            if bank == 0:
-                x_grouped[g] = work.tile([P, GROUP * PACK], BF16, align_bytes=64, name="x_grouped")
-            grouped_words = x_grouped[g][:].bitcast(F32)
-            nc.scalar.copy(
+        def new_x_tile(groups):
+            tile = work.tile([P, TURN, GROUP * PACK], BF16, align_bytes=64, name="x_grouped")
+            for place, g in enumerate(groups):
+                x_grouped[g] = (tile, place)
+
+        def copy_out(g, bank, copy):
+            tile, place = x_grouped[g]
+            grouped_words = tile[:, place, :].bitcast(F32)
+            copy(
                 out=grouped_words[:, bank * 4 * P : (bank + 1) * 4 * P].rearrange(
                     "q (s p u) -> q s p u", s=2, u=2
                 ),
                 in_=xt_banks[(g, bank)][:].rearrange("q s u p -> q s p u"),
             )
 
-        def quantise_x(g):
-            words = work.tile([P, GROUP], U32, align_bytes=64, name="x_words")
-            scales = work.tile([P, GROUP], U8, align_bytes=64, name="x_scales")
-            nc.vector.quantize_mx(out=words[:].bitcast(FP8X4), scales=scales[:], in_=x_grouped[g][:])
-            x_mx[g] = (words, scales)
+        def quantise_x(groups):
+            count = len(groups)
+            words = work.tile([P, TURN, GROUP], U32, align_bytes=64, name="x_words")
+            scales = work.tile([P, TURN, GROUP], U8, align_bytes=64, name="x_scales")
+            tile, place = x_grouped[groups[0]]
+            nc.vector.quantize_mx(
+                out=words[:, 0:count, :].rearrange("p g c -> p (g c)").bitcast(FP8X4),
+                scales=scales[:, 0:count, :].rearrange("p g c -> p (g c)"),
+                in_=tile[:, 0:count, :].rearrange("p g c -> p (g c)"),
+            )
+            for place, g in enumerate(groups):
+                x_mx[g] = (words[:, place, :], scales[:, place, :])
 
         def project_keys(g, block):
             words, scales = x_mx[g]
@@ -125,21 +142,23 @@ def tile_ufoattention_pa_t_kernel(tc, queries, Wk, bk, Wv, bv, gamma, out):
                 out=bank[:],
                 lhsT=w_words[:, cols].bitcast(FP8X4),
                 lhsT_scale=w_scales[:, cols],
-                rhs=words[:].bitcast(FP8X4),
-                rhs_scale=scales[:],
+                rhs=words.bitcast(FP8X4),
+                rhs_scale=scales,
                 start=True,
                 stop=True,
             )
             value_banks[(g, block)] = bank
 
+        def new_kv_tile(groups):
+            tile = work.tile([P, TURN, COLS * PACK], BF16, align_bytes=64, name="kv_grouped")
+            for place, g in enumerate(groups):
+                kv_grouped[g] = (tile, place)
+
         def add_key_bias(g, block):
-            if block == 0:
-                kv_grouped[g] = work.tile([P, COLS * PACK], BF16, align_bytes=64, name="kv_grouped")
+            tile, place = kv_grouped[g]
             first = block * BLOCK * PACK
             nc.vector.tensor_tensor(
-                out=kv_grouped[g][:, first : first + BLOCK * PACK].rearrange(
-                    "p (c t) -> p c t", t=PACK
-                ),
+                out=tile[:, place, first : first + BLOCK * PACK].rearrange("p (c t) -> p c t", t=PACK),
                 in0=key_banks[(g, block)][:].rearrange("p t c -> p c t"),
                 in1=key_bias[:, block_cols(block)].unsqueeze(2).to_broadcast([P, BLOCK, PACK]),
                 op=ADD,
@@ -155,37 +174,41 @@ def tile_ufoattention_pa_t_kernel(tc, queries, Wk, bk, Wv, bv, gamma, out):
                 scale=1.0,
             )
 
-        def transpose_back(g):
-            back = ring.tile([P, VALUE_BLOCKS, 2, BLOCK], F32, name="back", tag="ring")
-            for block in range(VALUE_BLOCKS):
+        def transpose_back(groups, block):
+            back = ring.tile([P, TURN, 2, BLOCK], F32, name="back", tag="ring")
+            for place, g in enumerate(groups):
                 pairs = rounded[(g, block)][:].bitcast(F32)
                 for u in range(2):
                     nc.tensor.transpose(
-                        back[:, block, u, :], pairs[:, u * P : (u + 1) * P], ident[:]
+                        back[:, place, u, :], pairs[:, u * P : (u + 1) * P], ident[:]
                     )
-            back_banks[g] = back
+            return back
 
-        def copy_back(g, block, copy):
-            first = (KEY_BLOCKS + block) * BLOCK * 2
+        def copy_back(groups, block, back, copy):
+            count = len(groups)
+            first = (KEY_BLOCKS + block) * BLOCK * PACK
+            tile, place = kv_grouped[groups[0]]
             copy(
-                out=kv_grouped[g][:]
-                .bitcast(F32)[:, first : first + BLOCK * 2]
-                .rearrange("p (c u) -> p c u", u=2),
-                in_=back_banks[g][:, block, :, :].rearrange("p u c -> p c u"),
+                out=tile[:, 0:count, first : first + BLOCK * PACK]
+                .bitcast(F32)
+                .rearrange("p g (c u) -> p g c u", u=2),
+                in_=back[:, 0:count, :, :].rearrange("p g u c -> p g c u"),
             )
 
-        def quantise_kv(g):
-            b, step = divmod(g, GROUPS_PER_BATCH)
+        def quantise_kv(groups):
+            count = len(groups)
+            b, step = divmod(groups[0], GROUPS_PER_BATCH)
             if step == 0:
                 kv_mx[b] = (
                     batch_pool.tile([P, GROUPS_PER_BATCH, COLS], U32, align_bytes=64, name="kv_words"),
                     batch_pool.tile([P, GROUPS_PER_BATCH, COLS], U8, align_bytes=64, name="kv_scales"),
                 )
             words, scales = kv_mx[b]
+            tile, place = kv_grouped[groups[0]]
             nc.vector.quantize_mx(
-                out=words[:, step, :].bitcast(FP8X4),
-                scales=scales[:, step, :],
-                in_=kv_grouped[g][:],
+                out=words[:, step : step + count, :].rearrange("p g c -> p (g c)").bitcast(FP8X4),
+                scales=scales[:, step : step + count, :].rearrange("p g c -> p (g c)"),
+                in_=tile[:, 0:count, :].rearrange("p g c -> p (g c)"),
             )
 
         def second_product(b, pair, step):
@@ -262,25 +285,20 @@ def tile_ufoattention_pa_t_kernel(tc, queries, Wk, bk, Wv, bv, gamma, out):
 
         last_batch = BATCHES - 1
         places = last_batch * HEAD_PAIRS
-        kv_all = consts.tile([P, places, BLOCK], F32)
+        kv_all = consts.tile([P, places, HEAD_DIM], F32)
         squares = consts.tile([P, HEAD_DIM], F32)
         sum_squares = consts.tile([P, places], F32)
         norms = consts.tile([P, last_batch, HEAD_PAIRS], F32)
         last_sum_squares = consts.tile([P, HEAD_PAIRS], F32)
 
-        def add_squares(product, accumulator):
-            for half in range(2):
-                rows = half_rows(half)
-                nc.scalar.activation(
-                    out=squares[rows, :],
-                    in_=product[rows, rows],
-                    func=ACT.Square,
-                    accum_out=accumulator[rows, :],
-                )
-
         def norms_of_first_batches():
             for place in range(places):
-                add_squares(kv_all[:, place, :], sum_squares[:, place : place + 1])
+                nc.scalar.activation(
+                    out=squares[:],
+                    in_=kv_all[:, place, :],
+                    func=ACT.Square,
+                    accum_out=sum_squares[:, place : place + 1],
+                )
             nc.scalar.activation(
                 out=norms[:].rearrange("p b pair -> p (b pair)"), in_=sum_squares[:], func=ACT.Sqrt
             )
@@ -304,21 +322,20 @@ def tile_ufoattention_pa_t_kernel(tc, queries, Wk, bk, Wv, bv, gamma, out):
                 op=MULT,
             )
             result = consts.tile([P, places, HEAD_DIM], F32)
-            for half in range(2):
-                rows = half_rows(half)
-                nc.vector.tensor_tensor(
-                    out=result[rows, :, :],
-                    in0=kv_all[rows, :, rows],
-                    in1=gains[rows, :, :]
-                    .rearrange("p b pair -> p (b pair)")
-                    .unsqueeze(2)
-                    .to_broadcast([HEAD_DIM, places, HEAD_DIM]),
-                    op=MULT,
-                )
+            nc.vector.tensor_tensor(
+                out=result[:],
+                in0=kv_all[:],
+                in1=gains[:]
+                .rearrange("p b pair -> p (b pair)")
+                .unsqueeze(2)
+                .to_broadcast([P, places, HEAD_DIM]),
+                op=MULT,
+            )
             nc.sync.dma_start(
                 out=out[0:last_batch].rearrange("b (pair half) i j -> (half i) (b pair) j", half=2),
                 in_=result[:],
             )
+
 
         turns = (
             [[0], [1]] + [[g, g + 1] for g in range(2, GROUPS - 2, 2)] + [[GROUPS - 2], [GROUPS - 1]]
@@ -352,42 +369,57 @@ def tile_ufoattention_pa_t_kernel(tc, queries, Wk, bk, Wv, bv, gamma, out):
                         kv_sums[(b, pair)] = kv_pool.tile([P, BLOCK], F32, name="kv_bank")
                 second_product(b, pair, step)
                 if step == GROUPS_PER_BATCH - 1 and b < last_batch:
-                    nc.scalar.copy(out=kv_all[:, b * HEAD_PAIRS + pair, :], in_=kv_sums[(b, pair)][:])
+                    for half in range(2):
+                        rows = half_rows(half)
+                        nc.scalar.copy(
+                            out=kv_all[rows, b * HEAD_PAIRS + pair, :],
+                            in_=kv_sums[(b, pair)][rows, rows],
+                        )
 
         for n in range(len(turns) + 3):
-            for g in groups_of(n - 1):
-                quantise_x(g)
-            for g in groups_of(n - 2):
-                for block in range(VALUE_BLOCKS):
+            x_groups, m_groups, k_groups = groups_of(n), groups_of(n - 2), groups_of(n - 3)
+            if groups_of(n - 1):
+                quantise_x(groups_of(n - 1))
+            if m_groups:
+                new_kv_tile(m_groups)
+            for block in range(VALUE_BLOCKS):
+                for g in m_groups:
                     project_values(g, block)
                     add_value_bias(g, block)
-            for g in groups_of(n - 2):
+            for g in m_groups:
                 for block in range(KEY_BLOCKS):
                     project_keys(g, block)
                     add_key_bias(g, block)
-            second_products(n, 2 * len(groups_of(n)) if n < len(turns) else len(passes))
-            if n == len(turns) + 1:
-                finish_first_batches()
-            for g in groups_of(n):
+            second_products(n, 2 * len(x_groups) if n < len(turns) else len(passes))
+            if x_groups:
+                new_x_tile(x_groups)
+            for g in x_groups:
                 transpose(g)
                 if g + X_BUFS < GROUPS:
                     load(g + X_BUFS)
-                copy_out(g, 0)
-                copy_out(g, 1)
-            for g in groups_of(n - 2):
-                transpose_back(g)
-            for g in groups_of(n - 3):
-                quantise_kv(g)
-                quantised[g] = n
-            for g in groups_of(n - 2):
-                copy_back(g, 0, nc.scalar.copy)
-                copy_back(g, 1, nc.vector.tensor_copy)
-            if n == len(turns):
-                norms_of_first_batches()
+                copy_out(g, 0, nc.scalar.copy)
+                copy_out(g, 1, nc.vector.tensor_copy if n < HEAD_TURNS else nc.scalar.copy)
+            if k_groups:
+                quantise_kv(k_groups)
+                for g in k_groups:
+                    quantised[g] = n
+            if m_groups:
+                backs = [transpose_back(m_groups, block) for block in range(VALUE_BLOCKS)]
+                copy_back(m_groups, 0, backs[0], nc.vector.tensor_copy)
+                copy_back(m_groups, 1, backs[1], nc.scalar.copy)
         second_products(len(turns) + 3, len(passes))
+        norms_of_first_batches()
+        finish_first_batches()
 
         for pair in range(HEAD_PAIRS):
-            add_squares(kv_sums[(last_batch, pair)], last_sum_squares[:, pair : pair + 1])
+            for half in range(2):
+                rows = half_rows(half)
+                nc.scalar.activation(
+                    out=squares[rows, :],
+                    in_=kv_sums[(last_batch, pair)][rows, rows],
+                    func=ACT.Square,
+                    accum_out=last_sum_squares[rows, pair : pair + 1],
+                )
         last_norms = consts.tile([P, HEAD_PAIRS], F32)
         nc.scalar.activation(out=last_norms[:], in_=last_sum_squares[:], func=ACT.Sqrt)
         last_gains = consts.tile([P, HEAD_PAIRS], F32)

@@ -27,7 +27,7 @@ KEY_BLOCKS = KEY_COLS // BLOCK
 VALUE_BLOCKS = BLOCKS - KEY_BLOCKS
 HEAD_PAIRS = HEADS // 2
 WORDS = FEATURES // 2
-HEAD_TURNS = 2
+HEAD_TURNS = 3
 TURN = 2
 X_BUFS = 8
 
@@ -225,17 +225,18 @@ def tile_ufoattention_pa_t_kernel(tc, queries, Wk, bk, Wv, bv, gamma, out):
                 stop=(step == GROUPS_PER_BATCH - 1),
             )
 
+        bias_row = consts.tile([P, COLS], BF16)
+        nc.vector.memset(bias_row[:], 0.0)
+        load(0)
         w_raw = consts.tile([P, 2, PACK, KEY_COLS], BF16)
         for which, w in enumerate((Wk, Wv)):
-            nc.scalar.dma_start(
+            nc.sync.dma_start(
                 out=w_raw[:, which, :, :].rearrange("q (u e) c -> q u (e c)", u=2),
                 in_=w.rearrange("(u q e) c -> q u (e c)", u=2, e=2),
             )
-        bias_row = consts.tile([P, COLS], BF16)
-        nc.vector.memset(bias_row[:], 0.0)
         nc.sync.dma_start(out=bias_row[0:1, 0:KEY_COLS], in_=bk.unsqueeze(0))
         nc.sync.dma_start(out=bias_row[0:1, KEY_COLS:COLS], in_=bv.unsqueeze(0))
-        for g in range(X_BUFS):
+        for g in range(1, X_BUFS):
             load(g)
 
         ident = consts.tile([P, P], F32)
@@ -250,38 +251,47 @@ def tile_ufoattention_pa_t_kernel(tc, queries, Wk, bk, Wv, bv, gamma, out):
         warm = consts.tile([P, 1], F32)
         nc.scalar.activation(out=warm[:], in_=one[:], func=ACT.Sqrt)
 
-        ones = consts.tile([P, P], BF16)
-        nc.vector.memset(ones[:], 1.0)
-        key_bias_bank = ring.tile([P, KEY_COLS], F32, name="key_bias_bank", tag="ring")
-        nc.tensor.matmul(
-            out=key_bias_bank[:], lhsT=ones[:], rhs=bias_row[:, 0:KEY_COLS], start=True, stop=True
-        )
-        key_bias = consts.tile([P, KEY_COLS], F32)
-        nc.scalar.copy(out=key_bias[:], in_=key_bias_bank[:])
-        value_bias_bank = ring.tile([P, VALUE_BLOCKS, HEAD_DIM], F32, name="value_bias_bank", tag="ring")
-        for block in range(VALUE_BLOCKS):
-            nc.tensor.matmul(
-                out=value_bias_bank[:, block, :],
-                lhsT=bias_row[:, block_cols(KEY_BLOCKS + block)],
-                rhs=ones[:, 0:HEAD_DIM],
-                start=True,
-                stop=True,
-            )
-        value_bias = consts.tile([P, VALUE_BLOCKS], F32)
-        nc.scalar.copy(out=value_bias[:], in_=value_bias_bank[:, :, 0])
-
         w_grouped = consts.tile([P, COLS, PACK], BF16, align_bytes=64)
-        nc.vector.tensor_copy(
-            out=w_grouped[:].rearrange("q (w c) t -> q w c t", w=2),
-            in_=w_raw[:].rearrange("q w t c -> q w c t"),
-        )
         w_words = consts.tile([P, COLS], U32, align_bytes=64)
         w_scales = consts.tile([P, COLS], U8, align_bytes=64)
-        nc.vector.quantize_mx(
-            out=w_words[:].bitcast(FP8X4),
-            scales=w_scales[:],
-            in_=w_grouped[:].rearrange("q c t -> q (c t)"),
-        )
+
+        ones = consts.tile([P, P], BF16)
+        nc.vector.memset(ones[:], 1.0)
+        key_bias = consts.tile([P, KEY_COLS], F32)
+        value_bias = consts.tile([P, VALUE_BLOCKS], F32)
+
+        def spread_biases():
+            key_bias_bank = ring.tile([P, KEY_COLS], F32, name="key_bias_bank", tag="ring")
+            nc.tensor.matmul(
+                out=key_bias_bank[:], lhsT=ones[:], rhs=bias_row[:, 0:KEY_COLS], start=True, stop=True
+            )
+            nc.scalar.copy(out=key_bias[:], in_=key_bias_bank[:])
+            value_bias_bank = ring.tile([P, VALUE_BLOCKS, HEAD_DIM], F32, name="value_bias_bank", tag="ring")
+            for block in range(VALUE_BLOCKS):
+                nc.tensor.matmul(
+                    out=value_bias_bank[:, block, :],
+                    lhsT=bias_row[:, block_cols(KEY_BLOCKS + block)],
+                    rhs=ones[:, 0:HEAD_DIM],
+                    start=True,
+                    stop=True,
+                )
+            nc.scalar.copy(out=value_bias[:], in_=value_bias_bank[:, :, 0])
+
+        def arrange_weights():
+            for which, copy in enumerate((nc.vector.tensor_copy, nc.scalar.copy)):
+                copy(
+                    out=w_grouped[:, which * KEY_COLS : (which + 1) * KEY_COLS, :],
+                    in_=w_raw[:, which, :, :].rearrange("q t c -> q c t"),
+                )
+
+        def quantise_weights():
+            for which in range(2):
+                cols = slice(which * KEY_COLS, (which + 1) * KEY_COLS)
+                nc.vector.quantize_mx(
+                    out=w_words[:, cols].bitcast(FP8X4),
+                    scales=w_scales[:, cols],
+                    in_=w_grouped[:, cols, :].rearrange("q c t -> q (c t)"),
+                )
 
         last_batch = BATCHES - 1
         places = last_batch * HEAD_PAIRS
@@ -375,11 +385,14 @@ def tile_ufoattention_pa_t_kernel(tc, queries, Wk, bk, Wv, bv, gamma, out):
                             out=kv_all[rows, b * HEAD_PAIRS + pair, :],
                             in_=kv_sums[(b, pair)][rows, rows],
                         )
+                    break
 
         for n in range(len(turns) + 3):
             x_groups, m_groups, k_groups = groups_of(n), groups_of(n - 2), groups_of(n - 3)
             if groups_of(n - 1):
                 quantise_x(groups_of(n - 1))
+            if n == 1:
+                quantise_weights()
             if m_groups:
                 new_kv_tile(m_groups)
             for block in range(VALUE_BLOCKS):
@@ -399,6 +412,9 @@ def tile_ufoattention_pa_t_kernel(tc, queries, Wk, bk, Wv, bv, gamma, out):
                     load(g + X_BUFS)
                 copy_out(g, 0, nc.scalar.copy)
                 copy_out(g, 1, nc.vector.tensor_copy if n < HEAD_TURNS else nc.scalar.copy)
+            if n == 0:
+                arrange_weights()
+                spread_biases()
             if k_groups:
                 quantise_kv(k_groups)
                 for g in k_groups:

@@ -24,7 +24,7 @@ COLS = 2 * KEY_COLS
 BLOCK = P
 BLOCKS = COLS // BLOCK
 KEY_BLOCKS = KEY_COLS // BLOCK
-VALUE_BLOCKS = BLOCKS - KEY_BLOCKS
+GPSIMD_BLOCK = BLOCKS - 1
 HEAD_PAIRS = HEADS // 2
 WORDS = FEATURES // 2
 HEAD_TURNS = 3
@@ -59,8 +59,7 @@ def tile_ufoattention_pa_t_kernel(tc, queries, Wk, bk, Wv, bv, gamma, out):
         xt_banks = {}
         x_grouped = {}
         x_mx = {}
-        key_banks = {}
-        value_banks = {}
+        banks = {}
         rounded = {}
         kv_grouped = {}
         kv_mx = {}
@@ -117,10 +116,10 @@ def tile_ufoattention_pa_t_kernel(tc, queries, Wk, bk, Wv, bv, gamma, out):
             for place, g in enumerate(groups):
                 x_mx[g] = (words[:, place, :], scales[:, place, :])
 
-        def project_keys(g, block):
+        def project(g, block):
             words, scales = x_mx[g]
             cols = block_cols(block)
-            bank = ring.tile([P, PACK, BLOCK], F32, name="key_bank", tag="ring")
+            bank = ring.tile([P, PACK, BLOCK], F32, name="bank", tag="ring")
             for t in range(PACK):
                 slot = slice(t * P, (t + 1) * P)
                 nc.tensor.matmul_mx(
@@ -132,12 +131,12 @@ def tile_ufoattention_pa_t_kernel(tc, queries, Wk, bk, Wv, bv, gamma, out):
                     start=True,
                     stop=True,
                 )
-            key_banks[(g, block)] = bank
+            banks[(g, block)] = bank
 
-        def project_values(g, block):
+        def project_turned(g, block):
             words, scales = x_mx[g]
-            cols = block_cols(KEY_BLOCKS + block)
-            bank = ring.tile([P, GROUP], F32, name="value_bank", tag="ring")
+            cols = block_cols(block)
+            bank = ring.tile([P, GROUP], F32, name="turned_bank", tag="ring")
             nc.tensor.matmul_mx(
                 out=bank[:],
                 lhsT=w_words[:, cols].bitcast(FP8X4),
@@ -147,30 +146,45 @@ def tile_ufoattention_pa_t_kernel(tc, queries, Wk, bk, Wv, bv, gamma, out):
                 start=True,
                 stop=True,
             )
-            value_banks[(g, block)] = bank
+            banks[(g, block)] = bank
 
         def new_kv_tile(groups):
             tile = work.tile([P, TURN, COLS * PACK], BF16, align_bytes=64, name="kv_grouped")
             for place, g in enumerate(groups):
                 kv_grouped[g] = (tile, place)
 
-        def add_key_bias(g, block):
+        def add_bias(g, block):
             tile, place = kv_grouped[g]
             first = block * BLOCK * PACK
             nc.vector.tensor_tensor(
                 out=tile[:, place, first : first + BLOCK * PACK].rearrange("p (c t) -> p c t", t=PACK),
-                in0=key_banks[(g, block)][:].rearrange("p t c -> p c t"),
-                in1=key_bias[:, block_cols(block)].unsqueeze(2).to_broadcast([P, BLOCK, PACK]),
+                in0=banks[(g, block)][:].rearrange("p t c -> p c t"),
+                in1=bias[:, block_cols(block)].unsqueeze(2).to_broadcast([P, BLOCK, PACK]),
                 op=ADD,
             )
 
-        def add_value_bias(g, block):
+        def add_bias_by_gpsimd(g, block):
+            tile, place = kv_grouped[g]
+            first = block * BLOCK * PACK
+            plain = work.tile([P, BLOCK * PACK], F32, name="plain")
+            nc.scalar.copy(
+                out=plain[:].rearrange("p (c t) -> p c t", t=PACK),
+                in_=banks[(g, block)][:].rearrange("p t c -> p c t"),
+            )
+            nc.gpsimd.tensor_tensor(
+                out=tile[:, place, first : first + BLOCK * PACK],
+                in0=plain[:],
+                in1=gpsimd_bias[:],
+                op=ADD,
+            )
+
+        def add_turned_bias(g, block):
             rounded[(g, block)] = work.tile([P, GROUP], BF16, name="rounded" + str(block))
             nc.scalar.activation(
                 out=rounded[(g, block)][:].rearrange("c (u p e) -> c u p e", u=2, e=2),
-                in_=value_banks[(g, block)][:].rearrange("c (u e p) -> c u p e", u=2, e=2),
+                in_=banks[(g, block)][:].rearrange("c (u e p) -> c u p e", u=2, e=2),
                 func=ACT.Identity,
-                bias=value_bias[:, block : block + 1],
+                bias=turned_bias[:, block : block + 1],
                 scale=1.0,
             )
 
@@ -186,7 +200,7 @@ def tile_ufoattention_pa_t_kernel(tc, queries, Wk, bk, Wv, bv, gamma, out):
 
         def copy_back(groups, block, back, copy):
             count = len(groups)
-            first = (KEY_BLOCKS + block) * BLOCK * PACK
+            first = block * BLOCK * PACK
             tile, place = kv_grouped[groups[0]]
             copy(
                 out=tile[:, 0:count, first : first + BLOCK * PACK]
@@ -257,25 +271,28 @@ def tile_ufoattention_pa_t_kernel(tc, queries, Wk, bk, Wv, bv, gamma, out):
 
         ones = consts.tile([P, P], BF16)
         nc.vector.memset(ones[:], 1.0)
-        key_bias = consts.tile([P, KEY_COLS], F32)
-        value_bias = consts.tile([P, VALUE_BLOCKS], F32)
+        bias = consts.tile([P, COLS], F32)
+        turned_bias = consts.tile([P, BLOCKS], F32)
+        gpsimd_bias = consts.tile([P, BLOCK * PACK], F32)
 
         def spread_biases():
-            key_bias_bank = ring.tile([P, KEY_COLS], F32, name="key_bias_bank", tag="ring")
-            nc.tensor.matmul(
-                out=key_bias_bank[:], lhsT=ones[:], rhs=bias_row[:, 0:KEY_COLS], start=True, stop=True
+            bias_bank = ring.tile([P, COLS], F32, name="bias_bank", tag="ring")
+            nc.tensor.matmul(out=bias_bank[:], lhsT=ones[:], rhs=bias_row[:], start=True, stop=True)
+            nc.scalar.copy(out=bias[:, 0:KEY_COLS], in_=bias_bank[:, 0:KEY_COLS])
+            nc.scalar.copy(
+                out=gpsimd_bias[:].rearrange("p (c t) -> p c t", t=PACK),
+                in_=bias_bank[:, block_cols(GPSIMD_BLOCK)].unsqueeze(2).to_broadcast([P, BLOCK, PACK]),
             )
-            nc.scalar.copy(out=key_bias[:], in_=key_bias_bank[:])
-            value_bias_bank = ring.tile([P, VALUE_BLOCKS, HEAD_DIM], F32, name="value_bias_bank", tag="ring")
-            for block in range(VALUE_BLOCKS):
+            turned_bias_bank = ring.tile([P, BLOCKS, HEAD_DIM], F32, name="turned_bias_bank", tag="ring")
+            for block in range(1, BLOCKS):
                 nc.tensor.matmul(
-                    out=value_bias_bank[:, block, :],
-                    lhsT=bias_row[:, block_cols(KEY_BLOCKS + block)],
+                    out=turned_bias_bank[:, block, :],
+                    lhsT=bias_row[:, block_cols(block)],
                     rhs=ones[:, 0:HEAD_DIM],
                     start=True,
                     stop=True,
                 )
-            nc.scalar.copy(out=value_bias[:], in_=value_bias_bank[:, :, 0])
+            nc.scalar.copy(out=turned_bias[:, 1:BLOCKS], in_=turned_bias_bank[:, 1:BLOCKS, 0])
 
         def arrange_weights():
             for which, copy in enumerate((nc.vector.tensor_copy, nc.scalar.copy)):
@@ -325,14 +342,14 @@ def tile_ufoattention_pa_t_kernel(tc, queries, Wk, bk, Wv, bv, gamma, out):
                 )
             gains = consts.tile([P, last_batch, HEAD_PAIRS], F32)
             nc.vector.reciprocal(out=gains[:], in_=norms[:])
-            nc.vector.tensor_tensor(
+            nc.gpsimd.tensor_tensor(
                 out=gains[:],
                 in0=gains[:],
                 in1=gamma_rows[:].unsqueeze(1).to_broadcast([P, last_batch, HEAD_PAIRS]),
                 op=MULT,
             )
             result = consts.tile([P, places, HEAD_DIM], F32)
-            nc.vector.tensor_tensor(
+            nc.gpsimd.tensor_tensor(
                 out=result[:],
                 in0=kv_all[:],
                 in1=gains[:]
@@ -350,6 +367,14 @@ def tile_ufoattention_pa_t_kernel(tc, queries, Wk, bk, Wv, bv, gamma, out):
         turns = (
             [[0], [1]] + [[g, g + 1] for g in range(2, GROUPS - 2, 2)] + [[GROUPS - 2], [GROUPS - 1]]
         )
+
+        seconds = [turn[1] for turn in turns if len(turn) > 1]
+
+        def gpsimd_blocks(g):
+            return (GPSIMD_BLOCK,) if g in seconds else ()
+
+        def turned_blocks(g):
+            return tuple(block for block in (2, 3) if block not in gpsimd_blocks(g))
 
         def groups_of(n):
             return turns[n] if 0 <= n < len(turns) else []
@@ -395,15 +420,22 @@ def tile_ufoattention_pa_t_kernel(tc, queries, Wk, bk, Wv, bv, gamma, out):
                 quantise_weights()
             if m_groups:
                 new_kv_tile(m_groups)
-            for block in range(VALUE_BLOCKS):
+            for block in range(BLOCKS):
                 for g in m_groups:
-                    project_values(g, block)
-                    add_value_bias(g, block)
+                    if block in turned_blocks(g):
+                        project_turned(g, block)
+                        add_turned_bias(g, block)
             for g in m_groups:
-                for block in range(KEY_BLOCKS):
-                    project_keys(g, block)
-                    add_key_bias(g, block)
-            second_products(n, 2 * len(x_groups) if n < len(turns) else len(passes))
+                for block in gpsimd_blocks(g):
+                    project(g, block)
+                    add_bias_by_gpsimd(g, block)
+            for g in m_groups:
+                for block in range(BLOCKS):
+                    if block not in turned_blocks(g) and block not in gpsimd_blocks(g):
+                        project(g, block)
+                        add_bias(g, block)
+            if n < len(turns):
+                second_products(n, 2 * len(x_groups))
             if x_groups:
                 new_x_tile(x_groups)
             for g in x_groups:
@@ -415,14 +447,20 @@ def tile_ufoattention_pa_t_kernel(tc, queries, Wk, bk, Wv, bv, gamma, out):
             if n == 0:
                 arrange_weights()
                 spread_biases()
+            tail = n >= len(turns)
+            backs = [
+                (block, [g for g in m_groups if block in turned_blocks(g)]) for block in range(BLOCKS)
+            ]
+            backs = [(block, groups, transpose_back(groups, block)) for block, groups in backs if groups]
+            if tail:
+                second_products(n, len(passes))
+            for place, (block, groups, back) in enumerate(backs):
+                by_vector = (place + n) % 2 == 0 and not tail
+                copy_back(groups, block, back, nc.vector.tensor_copy if by_vector else nc.scalar.copy)
             if k_groups:
                 quantise_kv(k_groups)
                 for g in k_groups:
                     quantised[g] = n
-            if m_groups:
-                backs = [transpose_back(m_groups, block) for block in range(VALUE_BLOCKS)]
-                copy_back(m_groups, 0, backs[0], nc.vector.tensor_copy)
-                copy_back(m_groups, 1, backs[1], nc.scalar.copy)
         second_products(len(turns) + 3, len(passes))
         norms_of_first_batches()
         finish_first_batches()

@@ -50,9 +50,9 @@ def tile_ufoattention_pa_t_kernel(tc, queries, Wk, bk, Wv, bv, gamma, out):
         consts = ctx.enter_context(tc.tile_pool(name="consts", bufs=1))
         x_pool = ctx.enter_context(tc.tile_pool(name="x", bufs=X_BUFS))
         work = ctx.enter_context(tc.tile_pool(name="work", bufs=3))
+        kv_tile_pool = ctx.enter_context(tc.tile_pool(name="kvt", bufs=2))
         batch_pool = ctx.enter_context(tc.tile_pool(name="batch", bufs=2))
-        ring = ctx.enter_context(tc.psum_pool(name="ring", bufs=7))
-        kv_pool = ctx.enter_context(tc.psum_pool(name="kv", bufs=1))
+        ring = ctx.enter_context(tc.psum_pool(name="ring", bufs=8))
         ctx.enter_context(tc.manual_schedule())
 
         x_tiles = {}
@@ -149,7 +149,7 @@ def tile_ufoattention_pa_t_kernel(tc, queries, Wk, bk, Wv, bv, gamma, out):
             banks[(g, block)] = bank
 
         def new_kv_tile(groups):
-            tile = work.tile([P, TURN, COLS * PACK], BF16, align_bytes=64, name="kv_grouped")
+            tile = kv_tile_pool.tile([P, TURN, COLS * PACK], BF16, align_bytes=64, name="kv_grouped")
             for place, g in enumerate(groups):
                 kv_grouped[g] = (tile, place)
 
@@ -163,18 +163,21 @@ def tile_ufoattention_pa_t_kernel(tc, queries, Wk, bk, Wv, bv, gamma, out):
                 op=ADD,
             )
 
-        def add_bias_by_gpsimd(g, block):
+        def copy_plain(g, block, plain):
             tile, place = kv_grouped[g]
-            first = block * BLOCK * PACK
-            plain = work.tile([P, BLOCK * PACK], F32, name="plain")
             nc.scalar.copy(
-                out=plain[:].rearrange("p (c t) -> p c t", t=PACK),
+                out=plain[:, place, :].rearrange("p (c t) -> p c t", t=PACK),
                 in_=banks[(g, block)][:].rearrange("p t c -> p c t"),
             )
+
+        def add_bias_by_gpsimd(groups, block, plain):
+            tile, place = kv_grouped[groups[0]]
+            first = block * BLOCK * PACK
+            count = len(groups)
             nc.gpsimd.tensor_tensor(
-                out=tile[:, place, first : first + BLOCK * PACK],
-                in0=plain[:],
-                in1=gpsimd_bias[:],
+                out=tile[:, 0:count, first : first + BLOCK * PACK],
+                in0=plain[:, 0:count, :],
+                in1=gpsimd_bias[:].unsqueeze(1).to_broadcast([P, count, BLOCK * PACK]),
                 op=ADD,
             )
 
@@ -203,7 +206,7 @@ def tile_ufoattention_pa_t_kernel(tc, queries, Wk, bk, Wv, bv, gamma, out):
             first = block * BLOCK * PACK
             tile, place = kv_grouped[groups[0]]
             copy(
-                out=tile[:, 0:count, first : first + BLOCK * PACK]
+                out=tile[:, place : place + count, first : first + BLOCK * PACK]
                 .bitcast(F32)
                 .rearrange("p g (c u) -> p g c u", u=2),
                 in_=back[:, 0:count, :, :].rearrange("p g u c -> p g c u"),
@@ -371,7 +374,7 @@ def tile_ufoattention_pa_t_kernel(tc, queries, Wk, bk, Wv, bv, gamma, out):
         seconds = [turn[1] for turn in turns if len(turn) > 1]
 
         def gpsimd_blocks(g):
-            return (GPSIMD_BLOCK,) if g in seconds else ()
+            return (GPSIMD_BLOCK,)
 
         def turned_blocks(g):
             return tuple(block for block in (2, 3) if block not in gpsimd_blocks(g))
@@ -388,20 +391,16 @@ def tile_ufoattention_pa_t_kernel(tc, queries, Wk, bk, Wv, bv, gamma, out):
                 passes += [(b, pair, s) for s in range(GROUPS_PER_BATCH) for pair in range(HEAD_PAIRS)]
 
         def second_products(n, limit):
-            while passes and limit > 0:
+            while passes:
                 b, pair, step = passes[0]
-                group = b * GROUPS_PER_BATCH + step
+                group = b * GROUPS_PER_BATCH + (step if b == last_batch else GROUPS_PER_BATCH - 1)
                 if group not in quantised or quantised[group] >= n:
                     break
                 if b == last_batch and n <= len(turns):
                     break
                 passes.remove(passes[0])
-                limit -= 1
                 if step == 0:
-                    if b == last_batch:
-                        kv_sums[(b, pair)] = ring.tile([P, BLOCK], F32, name="last_bank", tag="ring")
-                    else:
-                        kv_sums[(b, pair)] = kv_pool.tile([P, BLOCK], F32, name="kv_bank")
+                    kv_sums[(b, pair)] = ring.tile([P, BLOCK], F32, name="kv_bank", tag="ring")
                 second_product(b, pair, step)
                 if step == GROUPS_PER_BATCH - 1 and b < last_batch:
                     for half in range(2):
@@ -420,15 +419,17 @@ def tile_ufoattention_pa_t_kernel(tc, queries, Wk, bk, Wv, bv, gamma, out):
                 quantise_weights()
             if m_groups:
                 new_kv_tile(m_groups)
+            if m_groups:
+                plain = work.tile([P, TURN, BLOCK * PACK], F32, name="plain")
+                for g in m_groups:
+                    project(g, GPSIMD_BLOCK)
+                    copy_plain(g, GPSIMD_BLOCK, plain)
+                add_bias_by_gpsimd(m_groups, GPSIMD_BLOCK, plain)
             for block in range(BLOCKS):
                 for g in m_groups:
                     if block in turned_blocks(g):
                         project_turned(g, block)
                         add_turned_bias(g, block)
-            for g in m_groups:
-                for block in gpsimd_blocks(g):
-                    project(g, block)
-                    add_bias_by_gpsimd(g, block)
             for g in m_groups:
                 for block in range(BLOCKS):
                     if block not in turned_blocks(g) and block not in gpsimd_blocks(g):
@@ -449,13 +450,13 @@ def tile_ufoattention_pa_t_kernel(tc, queries, Wk, bk, Wv, bv, gamma, out):
                 spread_biases()
             tail = n >= len(turns)
             backs = [
-                (block, [g for g in m_groups if block in turned_blocks(g)]) for block in range(BLOCKS)
+                (block, [g]) for block in range(BLOCKS) for g in m_groups if block in turned_blocks(g)
             ]
             backs = [(block, groups, transpose_back(groups, block)) for block, groups in backs if groups]
             if tail:
                 second_products(n, len(passes))
             for place, (block, groups, back) in enumerate(backs):
-                by_vector = (place + n) % 2 == 0 and not tail
+                by_vector = place % 2 == 0 and not tail
                 copy_back(groups, block, back, nc.vector.tensor_copy if by_vector else nc.scalar.copy)
             if k_groups:
                 quantise_kv(k_groups)

@@ -149,33 +149,35 @@ def tile_ufoattention_pa_t_kernel(tc, queries, Wk, bk, Wv, bv, gamma, out):
             banks[(g, block)] = bank
 
         def new_kv_tile(groups):
-            tile = kv_tile_pool.tile([P, TURN, COLS * PACK], BF16, align_bytes=64, name="kv_grouped")
+            tile = kv_tile_pool.tile(
+                [P, BLOCKS * TURN * BLOCK * PACK], BF16, align_bytes=64, name="kv_grouped"
+            )
             for place, g in enumerate(groups):
-                kv_grouped[g] = (tile, place)
+                kv_grouped[g] = (tile, place, len(groups))
+
+        def kv_part(groups, block):
+            tile, place, count = kv_grouped[groups[0]]
+            first = block * count + place
+            return tile[:, first * BLOCK * PACK : (first + len(groups)) * BLOCK * PACK]
 
         def add_bias(g, block):
-            tile, place = kv_grouped[g]
-            first = block * BLOCK * PACK
             nc.vector.tensor_tensor(
-                out=tile[:, place, first : first + BLOCK * PACK].rearrange("p (c t) -> p c t", t=PACK),
+                out=kv_part([g], block).rearrange("p (c t) -> p c t", t=PACK),
                 in0=banks[(g, block)][:].rearrange("p t c -> p c t"),
                 in1=bias[:, block_cols(block)].unsqueeze(2).to_broadcast([P, BLOCK, PACK]),
                 op=ADD,
             )
 
-        def copy_plain(g, block, plain):
-            tile, place = kv_grouped[g]
+        def copy_plain(g, block, plain, place):
             nc.scalar.copy(
                 out=plain[:, place, :].rearrange("p (c t) -> p c t", t=PACK),
                 in_=banks[(g, block)][:].rearrange("p t c -> p c t"),
             )
 
         def add_bias_by_gpsimd(groups, block, plain):
-            tile, place = kv_grouped[groups[0]]
-            first = block * BLOCK * PACK
             count = len(groups)
             nc.gpsimd.tensor_tensor(
-                out=tile[:, 0:count, first : first + BLOCK * PACK],
+                out=kv_part(groups, block).rearrange("p (g e) -> p g e", g=count),
                 in0=plain[:, 0:count, :],
                 in1=gpsimd_bias[:].unsqueeze(1).to_broadcast([P, count, BLOCK * PACK]),
                 op=ADD,
@@ -202,14 +204,11 @@ def tile_ufoattention_pa_t_kernel(tc, queries, Wk, bk, Wv, bv, gamma, out):
             return back
 
         def copy_back(groups, block, back, copy):
-            count = len(groups)
-            first = block * BLOCK * PACK
-            tile, place = kv_grouped[groups[0]]
             copy(
-                out=tile[:, place : place + count, first : first + BLOCK * PACK]
+                out=kv_part(groups, block)
                 .bitcast(F32)
-                .rearrange("p g (c u) -> p g c u", u=2),
-                in_=back[:, 0:count, :, :].rearrange("p g u c -> p g c u"),
+                .rearrange("p (g c u) -> p g c u", g=len(groups), u=2),
+                in_=back[:, 0 : len(groups), :, :].rearrange("p g u c -> p g c u"),
             )
 
         def quantise_kv(groups):
@@ -217,27 +216,34 @@ def tile_ufoattention_pa_t_kernel(tc, queries, Wk, bk, Wv, bv, gamma, out):
             b, step = divmod(groups[0], GROUPS_PER_BATCH)
             if step == 0:
                 kv_mx[b] = (
-                    batch_pool.tile([P, GROUPS_PER_BATCH, COLS], U32, align_bytes=64, name="kv_words"),
-                    batch_pool.tile([P, GROUPS_PER_BATCH, COLS], U8, align_bytes=64, name="kv_scales"),
+                    batch_pool.tile([P, GROUPS_PER_BATCH * COLS], U32, align_bytes=64, name="kv_words"),
+                    batch_pool.tile([P, GROUPS_PER_BATCH * COLS], U8, align_bytes=64, name="kv_scales"),
                 )
             words, scales = kv_mx[b]
-            tile, place = kv_grouped[groups[0]]
+            cols = slice(step * COLS, (step + count) * COLS)
+            tile, place, count = kv_grouped[groups[0]]
             nc.vector.quantize_mx(
-                out=words[:, step : step + count, :].rearrange("p g c -> p (g c)").bitcast(FP8X4),
-                scales=scales[:, step : step + count, :].rearrange("p g c -> p (g c)"),
-                in_=tile[:, 0:count, :].rearrange("p g c -> p (g c)"),
+                out=words[:, cols].bitcast(FP8X4),
+                scales=scales[:, cols],
+                in_=tile[:, 0 : count * COLS * PACK],
             )
 
         def second_product(b, pair, step):
             words, scales = kv_mx[b]
-            k_cols = block_cols(pair)
-            v_cols = block_cols(KEY_BLOCKS + pair)
+            tile, place, count = kv_grouped[b * GROUPS_PER_BATCH + step]
+
+            def cols_of(block):
+                first = (step - place) * COLS + (block * count + place) * BLOCK
+                return slice(first, first + BLOCK)
+
+            k_cols = cols_of(pair)
+            v_cols = cols_of(HEAD_PAIRS + pair)
             nc.tensor.matmul_mx(
                 out=kv_sums[(b, pair)][:],
-                lhsT=words[:, step, k_cols].bitcast(FP8X4),
-                lhsT_scale=scales[:, step, k_cols],
-                rhs=words[:, step, v_cols].bitcast(FP8X4),
-                rhs_scale=scales[:, step, v_cols],
+                lhsT=words[:, k_cols].bitcast(FP8X4),
+                lhsT_scale=scales[:, k_cols],
+                rhs=words[:, v_cols].bitcast(FP8X4),
+                rhs_scale=scales[:, v_cols],
                 start=(step == 0),
                 stop=(step == GROUPS_PER_BATCH - 1),
             )
@@ -316,7 +322,7 @@ def tile_ufoattention_pa_t_kernel(tc, queries, Wk, bk, Wv, bv, gamma, out):
         last_batch = BATCHES - 1
         places = last_batch * HEAD_PAIRS
         kv_all = consts.tile([P, places, HEAD_DIM], F32)
-        squares = consts.tile([P, HEAD_DIM], F32)
+        squares = consts.tile([P, places + HEAD_PAIRS, HEAD_DIM], F32)
         sum_squares = consts.tile([P, places], F32)
         norms = consts.tile([P, last_batch, HEAD_PAIRS], F32)
         last_sum_squares = consts.tile([P, HEAD_PAIRS], F32)
@@ -324,7 +330,7 @@ def tile_ufoattention_pa_t_kernel(tc, queries, Wk, bk, Wv, bv, gamma, out):
         def norms_of_first_batches():
             for place in range(places):
                 nc.scalar.activation(
-                    out=squares[:],
+                    out=squares[:, place, :],
                     in_=kv_all[:, place, :],
                     func=ACT.Square,
                     accum_out=sum_squares[:, place : place + 1],
@@ -374,7 +380,7 @@ def tile_ufoattention_pa_t_kernel(tc, queries, Wk, bk, Wv, bv, gamma, out):
         seconds = [turn[1] for turn in turns if len(turn) > 1]
 
         def gpsimd_blocks(g):
-            return (GPSIMD_BLOCK,)
+            return (GPSIMD_BLOCK,) if g < GROUPS - 2 else ()
 
         def turned_blocks(g):
             return tuple(block for block in (2, 3) if block not in gpsimd_blocks(g))
@@ -419,11 +425,11 @@ def tile_ufoattention_pa_t_kernel(tc, queries, Wk, bk, Wv, bv, gamma, out):
                 quantise_weights()
             if m_groups:
                 new_kv_tile(m_groups)
-            if m_groups:
+            if m_groups and gpsimd_blocks(m_groups[0]):
                 plain = work.tile([P, TURN, BLOCK * PACK], F32, name="plain")
-                for g in m_groups:
+                for place, g in enumerate(m_groups):
                     project(g, GPSIMD_BLOCK)
-                    copy_plain(g, GPSIMD_BLOCK, plain)
+                    copy_plain(g, GPSIMD_BLOCK, plain, place)
                 add_bias_by_gpsimd(m_groups, GPSIMD_BLOCK, plain)
             for block in range(BLOCKS):
                 for g in m_groups:
@@ -470,7 +476,7 @@ def tile_ufoattention_pa_t_kernel(tc, queries, Wk, bk, Wv, bv, gamma, out):
             for half in range(2):
                 rows = half_rows(half)
                 nc.scalar.activation(
-                    out=squares[rows, :],
+                    out=squares[rows, places + pair, :],
                     in_=kv_sums[(last_batch, pair)][rows, rows],
                     func=ACT.Square,
                     accum_out=last_sum_squares[rows, pair : pair + 1],

@@ -50,7 +50,7 @@ def tile_ufoattention_pa_t_kernel(tc, queries, Wk, bk, Wv, bv, gamma, out):
         consts = ctx.enter_context(tc.tile_pool(name="consts", bufs=1))
         x_pool = ctx.enter_context(tc.tile_pool(name="x", bufs=X_BUFS))
         work = ctx.enter_context(tc.tile_pool(name="work", bufs=3))
-        kv_tile_pool = ctx.enter_context(tc.tile_pool(name="kvt", bufs=2))
+        kv_tile_pool = ctx.enter_context(tc.tile_pool(name="kvt", bufs=3))
         batch_pool = ctx.enter_context(tc.tile_pool(name="batch", bufs=2))
         ring = ctx.enter_context(tc.psum_pool(name="ring", bufs=8))
         ctx.enter_context(tc.manual_schedule())
@@ -155,9 +155,13 @@ def tile_ufoattention_pa_t_kernel(tc, queries, Wk, bk, Wv, bv, gamma, out):
             for place, g in enumerate(groups):
                 kv_grouped[g] = (tile, place, len(groups))
 
+        def kv_start(g, block):
+            tile, place, count = kv_grouped[g]
+            return (block % HEAD_PAIRS * 2 + block // HEAD_PAIRS) * count + place
+
         def kv_part(groups, block):
             tile, place, count = kv_grouped[groups[0]]
-            first = block * count + place
+            first = kv_start(groups[0], block)
             return tile[:, first * BLOCK * PACK : (first + len(groups)) * BLOCK * PACK]
 
         def add_bias(g, block):
@@ -211,8 +215,7 @@ def tile_ufoattention_pa_t_kernel(tc, queries, Wk, bk, Wv, bv, gamma, out):
                 in_=back[:, 0 : len(groups), :, :].rearrange("p g u c -> p g c u"),
             )
 
-        def quantise_kv(groups):
-            count = len(groups)
+        def quantise_kv(groups, parts):
             b, step = divmod(groups[0], GROUPS_PER_BATCH)
             if step == 0:
                 kv_mx[b] = (
@@ -220,20 +223,22 @@ def tile_ufoattention_pa_t_kernel(tc, queries, Wk, bk, Wv, bv, gamma, out):
                     batch_pool.tile([P, GROUPS_PER_BATCH * COLS], U8, align_bytes=64, name="kv_scales"),
                 )
             words, scales = kv_mx[b]
-            cols = slice(step * COLS, (step + count) * COLS)
             tile, place, count = kv_grouped[groups[0]]
-            nc.vector.quantize_mx(
-                out=words[:, cols].bitcast(FP8X4),
-                scales=scales[:, cols],
-                in_=tile[:, 0 : count * COLS * PACK],
-            )
+            width = count * COLS // parts
+            for part in range(parts):
+                first = step * COLS + part * width
+                nc.vector.quantize_mx(
+                    out=words[:, first : first + width].bitcast(FP8X4),
+                    scales=scales[:, first : first + width],
+                    in_=tile[:, part * width * PACK : (part + 1) * width * PACK],
+                )
 
         def second_product(b, pair, step):
             words, scales = kv_mx[b]
             tile, place, count = kv_grouped[b * GROUPS_PER_BATCH + step]
 
             def cols_of(block):
-                first = (step - place) * COLS + (block * count + place) * BLOCK
+                first = (step - place) * COLS + kv_start(b * GROUPS_PER_BATCH + step, block) * BLOCK
                 return slice(first, first + BLOCK)
 
             k_cols = cols_of(pair)
@@ -272,7 +277,7 @@ def tile_ufoattention_pa_t_kernel(tc, queries, Wk, bk, Wv, bv, gamma, out):
         one = consts.tile([P, 1], F32)
         nc.vector.memset(one[:], 1.0)
         warm = consts.tile([P, 1], F32)
-        nc.scalar.activation(out=warm[:], in_=one[:], func=ACT.Sqrt)
+        nc.scalar.activation(out=warm[:], in_=one[:], func=ACT.Abs_reciprocal_sqrt)
 
         w_grouped = consts.tile([P, COLS, PACK], BF16, align_bytes=64)
         w_words = consts.tile([P, COLS], U32, align_bytes=64)
@@ -324,8 +329,7 @@ def tile_ufoattention_pa_t_kernel(tc, queries, Wk, bk, Wv, bv, gamma, out):
         kv_all = consts.tile([P, places, HEAD_DIM], F32)
         squares = consts.tile([P, places + HEAD_PAIRS, HEAD_DIM], F32)
         sum_squares = consts.tile([P, places], F32)
-        norms = consts.tile([P, last_batch, HEAD_PAIRS], F32)
-        last_sum_squares = consts.tile([P, HEAD_PAIRS], F32)
+        inverse_norms = consts.tile([P, last_batch, HEAD_PAIRS], F32)
 
         def norms_of_first_batches():
             for place in range(places):
@@ -336,29 +340,30 @@ def tile_ufoattention_pa_t_kernel(tc, queries, Wk, bk, Wv, bv, gamma, out):
                     accum_out=sum_squares[:, place : place + 1],
                 )
             nc.scalar.activation(
-                out=norms[:].rearrange("p b pair -> p (b pair)"), in_=sum_squares[:], func=ACT.Sqrt
+                out=inverse_norms[:].rearrange("p b pair -> p (b pair)"),
+                in_=sum_squares[:],
+                func=ACT.Abs_reciprocal_sqrt,
             )
 
         gamma_rows = consts.tile([P, HEAD_PAIRS], F32)
+        for half in range(2):
+            nc.gpsimd.tensor_copy(
+                out=gamma_rows[half_rows(half), :],
+                in_=gamma_bf[half_rows(half), :].rearrange("p (pair half) -> p half pair", half=2)[
+                    :, half, :
+                ],
+            )
 
         def finish_first_batches():
-            for half in range(2):
-                nc.vector.tensor_copy(
-                    out=gamma_rows[half_rows(half), :],
-                    in_=gamma_bf[half_rows(half), :].rearrange("p (pair half) -> p half pair", half=2)[
-                        :, half, :
-                    ],
-                )
             gains = consts.tile([P, last_batch, HEAD_PAIRS], F32)
-            nc.vector.reciprocal(out=gains[:], in_=norms[:])
-            nc.gpsimd.tensor_tensor(
+            nc.vector.tensor_tensor(
                 out=gains[:],
-                in0=gains[:],
+                in0=inverse_norms[:],
                 in1=gamma_rows[:].unsqueeze(1).to_broadcast([P, last_batch, HEAD_PAIRS]),
                 op=MULT,
             )
             result = consts.tile([P, places, HEAD_DIM], F32)
-            nc.gpsimd.tensor_tensor(
+            nc.vector.tensor_tensor(
                 out=result[:],
                 in0=kv_all[:],
                 in1=gains[:]
@@ -383,7 +388,8 @@ def tile_ufoattention_pa_t_kernel(tc, queries, Wk, bk, Wv, bv, gamma, out):
             return (GPSIMD_BLOCK,) if g < GROUPS - 2 else ()
 
         def turned_blocks(g):
-            return tuple(block for block in (2, 3) if block not in gpsimd_blocks(g))
+            blocks = (1, 2, 3) if g == GROUPS - 2 else (2, 3)
+            return tuple(block for block in blocks if block not in gpsimd_blocks(g))
 
         def groups_of(n):
             return turns[n] if 0 <= n < len(turns) else []
@@ -411,7 +417,8 @@ def tile_ufoattention_pa_t_kernel(tc, queries, Wk, bk, Wv, bv, gamma, out):
                 if step == GROUPS_PER_BATCH - 1 and b < last_batch:
                     for half in range(2):
                         rows = half_rows(half)
-                        nc.scalar.copy(
+                        copy = (nc.scalar.copy, nc.vector.tensor_copy)[half]
+                        copy(
                             out=kv_all[rows, b * HEAD_PAIRS + pair, :],
                             in_=kv_sums[(b, pair)][rows, rows],
                         )
@@ -465,7 +472,7 @@ def tile_ufoattention_pa_t_kernel(tc, queries, Wk, bk, Wv, bv, gamma, out):
                 by_vector = place % 2 == 0 and not tail
                 copy_back(groups, block, back, nc.vector.tensor_copy if by_vector else nc.scalar.copy)
             if k_groups:
-                quantise_kv(k_groups)
+                quantise_kv(k_groups, HEAD_PAIRS if GROUPS - 1 in k_groups else 1)
                 for g in k_groups:
                     quantised[g] = n
         second_products(len(turns) + 3, len(passes))
@@ -473,31 +480,32 @@ def tile_ufoattention_pa_t_kernel(tc, queries, Wk, bk, Wv, bv, gamma, out):
         finish_first_batches()
 
         for pair in range(HEAD_PAIRS):
+            sums = kv_sums[(last_batch, pair)]
+            pair_sum_squares = consts.tile([P, 1], F32, name="pair_sum_squares" + str(pair))
             for half in range(2):
                 rows = half_rows(half)
                 nc.scalar.activation(
                     out=squares[rows, places + pair, :],
-                    in_=kv_sums[(last_batch, pair)][rows, rows],
+                    in_=sums[rows, rows],
                     func=ACT.Square,
-                    accum_out=last_sum_squares[rows, pair : pair + 1],
+                    accum_out=pair_sum_squares[rows, :],
                 )
-        last_norms = consts.tile([P, HEAD_PAIRS], F32)
-        nc.scalar.activation(out=last_norms[:], in_=last_sum_squares[:], func=ACT.Sqrt)
-        last_gains = consts.tile([P, HEAD_PAIRS], F32)
-        nc.vector.reciprocal(out=last_gains[:], in_=last_norms[:])
-        last_result = consts.tile([P, HEAD_PAIRS, HEAD_DIM], F32)
-        for pair in range(HEAD_PAIRS):
+            pair_inverse_norms = consts.tile([P, 1], F32, name="pair_inverse_norms" + str(pair))
+            nc.scalar.activation(
+                out=pair_inverse_norms[:], in_=pair_sum_squares[:], func=ACT.Abs_reciprocal_sqrt
+            )
+            pair_result = consts.tile([P, HEAD_DIM], F32, name="pair_result" + str(pair))
             for half in range(2):
                 rows = half_rows(half)
                 nc.vector.tensor_scalar(
-                    out=last_result[rows, pair, :],
-                    in0=kv_sums[(last_batch, pair)][rows, rows],
-                    scalar1=last_gains[rows, pair : pair + 1],
+                    out=pair_result[rows, :],
+                    in0=sums[rows, rows],
+                    scalar1=pair_inverse_norms[rows, :],
                     scalar2=gamma_rows[rows, pair : pair + 1],
                     op0=MULT,
                     op1=MULT,
                 )
-        nc.sync.dma_start(
-            out=out[last_batch].rearrange("(pair half) i j -> (half i) pair j", half=2),
-            in_=last_result[:],
-        )
+            nc.sync.dma_start(
+                out=out[last_batch, pair * 2 : (pair + 1) * 2].rearrange("half i j -> (half i) j"),
+                in_=pair_result[:],
+            )

from contextlib import ExitStack

import concourse.mybir as mybir
from concourse.masks import make_identity

BF16 = mybir.dt.bfloat16
F32 = mybir.dt.float32
U32 = mybir.dt.uint32
U8 = mybir.dt.uint8
FP8X4 = mybir.dt.float8_e4m3fn_x4
ADD = mybir.AluOpType.add
MULT = mybir.AluOpType.mult
ACT = mybir.ActivationFunctionType

BATCHES, TOKENS_PER_BATCH, FEATURES, HEADS, HEAD_DIM = 4, 4096, 512, 4, 64

P = 128
PACK = 4
GROUP = P * PACK
GROUPS = BATCHES * TOKENS_PER_BATCH // GROUP
GROUPS_PER_BATCH = TOKENS_PER_BATCH // GROUP
KEY_COLS = HEADS * HEAD_DIM
COLS = 2 * KEY_COLS
BLOCK = P
BLOCKS = COLS // BLOCK
KEY_BLOCKS = KEY_COLS // BLOCK
GPSIMD_BLOCK = BLOCKS - 1
HEAD_PAIRS = HEADS // 2
WORDS = FEATURES // 2
HEAD_TURNS = 3
TURN = 2
X_BUFS = 8

FLOPS = 2 * BATCHES * TOKENS_PER_BATCH * (FEATURES * COLS + HEADS * HEAD_DIM * HEAD_DIM)


def block_cols(block):
    return slice(block * BLOCK, (block + 1) * BLOCK)


def half_rows(half):
    return slice(half * HEAD_DIM, (half + 1) * HEAD_DIM)


def tile_ufoattention_pa_t_kernel(tc, queries, Wk, bk, Wv, bv, gamma, out):
    nc = tc.nc
    tokens = queries.flatten_outer_dims()

    with ExitStack() as ctx:
        consts = ctx.enter_context(tc.tile_pool(name="consts", bufs=1))
        x_pool = ctx.enter_context(tc.tile_pool(name="x", bufs=X_BUFS))
        work = ctx.enter_context(tc.tile_pool(name="work", bufs=3))
        kv_tile_pool = ctx.enter_context(tc.tile_pool(name="kvt", bufs=3))
        batch_pool = ctx.enter_context(tc.tile_pool(name="batch", bufs=2))
        ring = ctx.enter_context(tc.psum_pool(name="ring", bufs=8))
        ctx.enter_context(tc.manual_schedule())

        x_tiles = {}
        xt_banks = {}
        x_grouped = {}
        x_mx = {}
        banks = {}
        rounded = {}
        kv_grouped = {}
        kv_mx = {}
        kv_sums = {}

        def load(g):
            x_sb = x_pool.tile([P, PACK * FEATURES], BF16)
            pieces = 2 if g == 0 else 1
            for piece in range(pieces):
                part = slice(piece * PACK // pieces * FEATURES, (piece + 1) * PACK // pieces * FEATURES)
                nc.sync.dma_start(
                    out=x_sb[:, part],
                    in_=tokens[g * GROUP : (g + 1) * GROUP, :].rearrange("(p t) d -> p (t d)", t=PACK)[
                        :, part
                    ],
                )
            x_tiles[g] = x_sb

        def transpose(g):
            x_words = x_tiles[g][:].bitcast(F32)
            for bank in range(2):
                xt = ring.tile([P, 2, 2, P], F32, name="xt", tag="ring")
                for s in range(2):
                    for u in range(2):
                        first = ((2 * bank + s) * 2 + u) * P
                        nc.tensor.transpose(xt[:, s, u, :], x_words[:, first : first + P], ident[:])
                xt_banks[(g, bank)] = xt

        def new_x_tile(groups):
            tile = work.tile([P, TURN, GROUP * PACK], BF16, align_bytes=64, name="x_grouped")
            for place, g in enumerate(groups):
                x_grouped[g] = (tile, place)

        def copy_out(g, bank, copy):
            tile, place = x_grouped[g]
            grouped_words = tile[:, place, :].bitcast(F32)
            copy(
                out=grouped_words[:, bank * 4 * P : (bank + 1) * 4 * P].rearrange(
                    "q (s p u) -> q s p u", s=2, u=2
                ),
                in_=xt_banks[(g, bank)][:].rearrange("q s u p -> q s p u"),
            )

        def quantise_x(groups):
            count = len(groups)
            words = work.tile([P, TURN, GROUP], U32, align_bytes=64, name="x_words")
            scales = work.tile([P, TURN, GROUP], U8, align_bytes=64, name="x_scales")
            tile, place = x_grouped[groups[0]]
            nc.vector.quantize_mx(
                out=words[:, 0:count, :].rearrange("p g c -> p (g c)").bitcast(FP8X4),
                scales=scales[:, 0:count, :].rearrange("p g c -> p (g c)"),
                in_=tile[:, 0:count, :].rearrange("p g c -> p (g c)"),
            )
            for place, g in enumerate(groups):
                x_mx[g] = (words[:, place, :], scales[:, place, :])

        def project(g, block):
            words, scales = x_mx[g]
            cols = block_cols(block)
            bank = ring.tile([P, PACK, BLOCK], F32, name="bank", tag="ring")
            for t in range(PACK):
                slot = slice(t * P, (t + 1) * P)
                nc.tensor.matmul_mx(
                    out=bank[:, t, :],
                    lhsT=words[:, slot].bitcast(FP8X4),
                    lhsT_scale=scales[:, slot],
                    rhs=w_words[:, cols].bitcast(FP8X4),
                    rhs_scale=w_scales[:, cols],
                    start=True,
                    stop=True,
                )
            banks[(g, block)] = bank

        def project_turned(g, block):
            words, scales = x_mx[g]
            cols = block_cols(block)
            bank = ring.tile([P, GROUP], F32, name="turned_bank", tag="ring")
            nc.tensor.matmul_mx(
                out=bank[:],
                lhsT=w_words[:, cols].bitcast(FP8X4),
                lhsT_scale=w_scales[:, cols],
                rhs=words.bitcast(FP8X4),
                rhs_scale=scales,
                start=True,
                stop=True,
            )
            banks[(g, block)] = bank

        def new_kv_tile(groups):
            tile = kv_tile_pool.tile(
                [P, BLOCKS * TURN * BLOCK * PACK], BF16, align_bytes=64, name="kv_grouped"
            )
            for place, g in enumerate(groups):
                kv_grouped[g] = (tile, place, len(groups))

        def kv_start(g, block):
            tile, place, count = kv_grouped[g]
            return (block % HEAD_PAIRS * 2 + block // HEAD_PAIRS) * count + place

        def kv_part(groups, block):
            tile, place, count = kv_grouped[groups[0]]
            first = kv_start(groups[0], block)
            return tile[:, first * BLOCK * PACK : (first + len(groups)) * BLOCK * PACK]

        def add_bias(g, block):
            nc.vector.tensor_tensor(
                out=kv_part([g], block).rearrange("p (c t) -> p c t", t=PACK),
                in0=banks[(g, block)][:].rearrange("p t c -> p c t"),
                in1=bias[:, block_cols(block)].unsqueeze(2).to_broadcast([P, BLOCK, PACK]),
                op=ADD,
            )

        def copy_plain(g, block, plain, place):
            nc.scalar.copy(
                out=plain[:, place, :].rearrange("p (c t) -> p c t", t=PACK),
                in_=banks[(g, block)][:].rearrange("p t c -> p c t"),
            )

        def add_bias_by_gpsimd(groups, block, plain):
            count = len(groups)
            nc.gpsimd.tensor_tensor(
                out=kv_part(groups, block).rearrange("p (g e) -> p g e", g=count),
                in0=plain[:, 0:count, :],
                in1=gpsimd_bias[:].unsqueeze(1).to_broadcast([P, count, BLOCK * PACK]),
                op=ADD,
            )

        def add_turned_bias(g, block):
            rounded[(g, block)] = work.tile([P, GROUP], BF16, name="rounded" + str(block))
            nc.scalar.activation(
                out=rounded[(g, block)][:].rearrange("c (u p e) -> c u p e", u=2, e=2),
                in_=banks[(g, block)][:].rearrange("c (u e p) -> c u p e", u=2, e=2),
                func=ACT.Identity,
                bias=turned_bias[:, block : block + 1],
                scale=1.0,
            )

        def transpose_back(groups, block):
            back = ring.tile([P, TURN, 2, BLOCK], F32, name="back", tag="ring")
            for place, g in enumerate(groups):
                pairs = rounded[(g, block)][:].bitcast(F32)
                for u in range(2):
                    nc.tensor.transpose(
                        back[:, place, u, :], pairs[:, u * P : (u + 1) * P], ident[:]
                    )
            return back

        def copy_back(groups, block, back, copy):
            copy(
                out=kv_part(groups, block)
                .bitcast(F32)
                .rearrange("p (g c u) -> p g c u", g=len(groups), u=2),
                in_=back[:, 0 : len(groups), :, :].rearrange("p g u c -> p g c u"),
            )

        def quantise_kv(groups, parts):
            b, step = divmod(groups[0], GROUPS_PER_BATCH)
            if step == 0:
                kv_mx[b] = (
                    batch_pool.tile([P, GROUPS_PER_BATCH * COLS], U32, align_bytes=64, name="kv_words"),
                    batch_pool.tile([P, GROUPS_PER_BATCH * COLS], U8, align_bytes=64, name="kv_scales"),
                )
            words, scales = kv_mx[b]
            tile, place, count = kv_grouped[groups[0]]
            width = count * COLS // parts
            for part in range(parts):
                first = step * COLS + part * width
                nc.vector.quantize_mx(
                    out=words[:, first : first + width].bitcast(FP8X4),
                    scales=scales[:, first : first + width],
                    in_=tile[:, part * width * PACK : (part + 1) * width * PACK],
                )

        def second_product(b, pair, step):
            words, scales = kv_mx[b]
            tile, place, count = kv_grouped[b * GROUPS_PER_BATCH + step]

            def cols_of(block):
                first = (step - place) * COLS + kv_start(b * GROUPS_PER_BATCH + step, block) * BLOCK
                return slice(first, first + BLOCK)

            k_cols = cols_of(pair)
            v_cols = cols_of(HEAD_PAIRS + pair)
            nc.tensor.matmul_mx(
                out=kv_sums[(b, pair)][:],
                lhsT=words[:, k_cols].bitcast(FP8X4),
                lhsT_scale=scales[:, k_cols],
                rhs=words[:, v_cols].bitcast(FP8X4),
                rhs_scale=scales[:, v_cols],
                start=(step == 0),
                stop=(step == GROUPS_PER_BATCH - 1),
            )

        bias_row = consts.tile([P, COLS], BF16)
        nc.vector.memset(bias_row[:], 0.0)
        load(0)
        w_raw = consts.tile([P, 2, PACK, KEY_COLS], BF16)
        for which, w in enumerate((Wk, Wv)):
            nc.sync.dma_start(
                out=w_raw[:, which, :, :].rearrange("q (u e) c -> q u (e c)", u=2),
                in_=w.rearrange("(u q e) c -> q u (e c)", u=2, e=2),
            )
        nc.sync.dma_start(out=bias_row[0:1, 0:KEY_COLS], in_=bk.unsqueeze(0))
        nc.sync.dma_start(out=bias_row[0:1, KEY_COLS:COLS], in_=bv.unsqueeze(0))
        for g in range(1, X_BUFS):
            load(g)

        ident = consts.tile([P, P], F32)
        make_identity(nc, ident[:])
        gamma_bf = consts.tile([P, HEADS], BF16)
        nc.gpsimd.dma_start(
            out=gamma_bf[:], in_=gamma.rearrange("o h x y -> (o h x y)").partition_broadcast(P)
        )

        one = consts.tile([P, 1], F32)
        nc.vector.memset(one[:], 1.0)
        warm = consts.tile([P, 1], F32)
        nc.scalar.activation(out=warm[:], in_=one[:], func=ACT.Abs_reciprocal_sqrt)

        w_grouped = consts.tile([P, COLS, PACK], BF16, align_bytes=64)
        w_words = consts.tile([P, COLS], U32, align_bytes=64)
        w_scales = consts.tile([P, COLS], U8, align_bytes=64)

        ones = consts.tile([P, P], BF16)
        nc.vector.memset(ones[:], 1.0)
        bias = consts.tile([P, COLS], F32)
        turned_bias = consts.tile([P, BLOCKS], F32)
        gpsimd_bias = consts.tile([P, BLOCK * PACK], F32)

        def spread_biases():
            bias_bank = ring.tile([P, COLS], F32, name="bias_bank", tag="ring")
            nc.tensor.matmul(out=bias_bank[:], lhsT=ones[:], rhs=bias_row[:], start=True, stop=True)
            nc.scalar.copy(out=bias[:, 0:KEY_COLS], in_=bias_bank[:, 0:KEY_COLS])
            nc.scalar.copy(
                out=gpsimd_bias[:].rearrange("p (c t) -> p c t", t=PACK),
                in_=bias_bank[:, block_cols(GPSIMD_BLOCK)].unsqueeze(2).to_broadcast([P, BLOCK, PACK]),
            )
            turned_bias_bank = ring.tile([P, BLOCKS, HEAD_DIM], F32, name="turned_bias_bank", tag="ring")
            for block in range(1, BLOCKS):
                nc.tensor.matmul(
                    out=turned_bias_bank[:, block, :],
                    lhsT=bias_row[:, block_cols(block)],
                    rhs=ones[:, 0:HEAD_DIM],
                    start=True,
                    stop=True,
                )
            nc.scalar.copy(out=turned_bias[:, 1:BLOCKS], in_=turned_bias_bank[:, 1:BLOCKS, 0])

        def arrange_weights():
            for which, copy in enumerate((nc.vector.tensor_copy, nc.scalar.copy)):
                copy(
                    out=w_grouped[:, which * KEY_COLS : (which + 1) * KEY_COLS, :],
                    in_=w_raw[:, which, :, :].rearrange("q t c -> q c t"),
                )

        def quantise_weights():
            for which in range(2):
                cols = slice(which * KEY_COLS, (which + 1) * KEY_COLS)
                nc.vector.quantize_mx(
                    out=w_words[:, cols].bitcast(FP8X4),
                    scales=w_scales[:, cols],
                    in_=w_grouped[:, cols, :].rearrange("q c t -> q (c t)"),
                )

        last_batch = BATCHES - 1
        places = last_batch * HEAD_PAIRS
        kv_all = consts.tile([P, places, HEAD_DIM], F32)
        squares = consts.tile([P, places + HEAD_PAIRS, HEAD_DIM], F32)
        sum_squares = consts.tile([P, places], F32)
        inverse_norms = consts.tile([P, last_batch, HEAD_PAIRS], F32)

        def norms_of_first_batches():
            for place in range(places):
                nc.scalar.activation(
                    out=squares[:, place, :],
                    in_=kv_all[:, place, :],
                    func=ACT.Square,
                    accum_out=sum_squares[:, place : place + 1],
                )
            nc.scalar.activation(
                out=inverse_norms[:].rearrange("p b pair -> p (b pair)"),
                in_=sum_squares[:],
                func=ACT.Abs_reciprocal_sqrt,
            )

        gamma_rows = consts.tile([P, HEAD_PAIRS], F32)
        for half in range(2):
            nc.gpsimd.tensor_copy(
                out=gamma_rows[half_rows(half), :],
                in_=gamma_bf[half_rows(half), :].rearrange("p (pair half) -> p half pair", half=2)[
                    :, half, :
                ],
            )

        def finish_first_batches():
            gains = consts.tile([P, last_batch, HEAD_PAIRS], F32)
            nc.vector.tensor_tensor(
                out=gains[:],
                in0=inverse_norms[:],
                in1=gamma_rows[:].unsqueeze(1).to_broadcast([P, last_batch, HEAD_PAIRS]),
                op=MULT,
            )
            result = consts.tile([P, places, HEAD_DIM], F32)
            nc.vector.tensor_tensor(
                out=result[:],
                in0=kv_all[:],
                in1=gains[:]
                .rearrange("p b pair -> p (b pair)")
                .unsqueeze(2)
                .to_broadcast([P, places, HEAD_DIM]),
                op=MULT,
            )
            nc.sync.dma_start(
                out=out[0:last_batch].rearrange("b (pair half) i j -> (half i) (b pair) j", half=2),
                in_=result[:],
            )


        turns = (
            [[0], [1]] + [[g, g + 1] for g in range(2, GROUPS - 2, 2)] + [[GROUPS - 2], [GROUPS - 1]]
        )

        seconds = [turn[1] for turn in turns if len(turn) > 1]

        def gpsimd_blocks(g):
            return (GPSIMD_BLOCK,) if g < GROUPS - 2 else ()

        def turned_blocks(g):
            blocks = (1, 2, 3) if g == GROUPS - 2 else (2, 3)
            return tuple(block for block in blocks if block not in gpsimd_blocks(g))

        def groups_of(n):
            return turns[n] if 0 <= n < len(turns) else []

        quantised = {}
        passes = []
        for b in range(BATCHES):
            if b < last_batch:
                passes += [(b, pair, s) for pair in range(HEAD_PAIRS) for s in range(GROUPS_PER_BATCH)]
            else:
                passes += [(b, pair, s) for s in range(GROUPS_PER_BATCH) for pair in range(HEAD_PAIRS)]

        def second_products(n, limit):
            while passes:
                b, pair, step = passes[0]
                group = b * GROUPS_PER_BATCH + (step if b == last_batch else GROUPS_PER_BATCH - 1)
                if group not in quantised or quantised[group] >= n:
                    break
                if b == last_batch and n <= len(turns):
                    break
                passes.remove(passes[0])
                if step == 0:
                    kv_sums[(b, pair)] = ring.tile([P, BLOCK], F32, name="kv_bank", tag="ring")
                second_product(b, pair, step)
                if step == GROUPS_PER_BATCH - 1 and b < last_batch:
                    for half in range(2):
                        rows = half_rows(half)
                        copy = (nc.scalar.copy, nc.vector.tensor_copy)[half]
                        copy(
                            out=kv_all[rows, b * HEAD_PAIRS + pair, :],
                            in_=kv_sums[(b, pair)][rows, rows],
                        )
                    break

        for n in range(len(turns) + 3):
            x_groups, m_groups, k_groups = groups_of(n), groups_of(n - 2), groups_of(n - 3)
            if groups_of(n - 1):
                quantise_x(groups_of(n - 1))
            if n == 1:
                quantise_weights()
            if m_groups:
                new_kv_tile(m_groups)
            if m_groups and gpsimd_blocks(m_groups[0]):
                plain = work.tile([P, TURN, BLOCK * PACK], F32, name="plain")
                for place, g in enumerate(m_groups):
                    project(g, GPSIMD_BLOCK)
                    copy_plain(g, GPSIMD_BLOCK, plain, place)
                add_bias_by_gpsimd(m_groups, GPSIMD_BLOCK, plain)
            for block in range(BLOCKS):
                for g in m_groups:
                    if block in turned_blocks(g):
                        project_turned(g, block)
                        add_turned_bias(g, block)
            for g in m_groups:
                for block in range(BLOCKS):
                    if block not in turned_blocks(g) and block not in gpsimd_blocks(g):
                        project(g, block)
                        add_bias(g, block)
            if n < len(turns):
                second_products(n, 2 * len(x_groups))
            if x_groups:
                new_x_tile(x_groups)
            for g in x_groups:
                transpose(g)
                if g + X_BUFS < GROUPS:
                    load(g + X_BUFS)
                copy_out(g, 0, nc.scalar.copy)
                copy_out(g, 1, nc.vector.tensor_copy if n < HEAD_TURNS else nc.scalar.copy)
            if n == 0:
                arrange_weights()
                spread_biases()
            tail = n >= len(turns)
            backs = [
                (block, [g]) for block in range(BLOCKS) for g in m_groups if block in turned_blocks(g)
            ]
            backs = [(block, groups, transpose_back(groups, block)) for block, groups in backs if groups]
            if tail:
                second_products(n, len(passes))
            for place, (block, groups, back) in enumerate(backs):
                by_vector = place % 2 == 0 and not tail
                copy_back(groups, block, back, nc.vector.tensor_copy if by_vector else nc.scalar.copy)
            if k_groups:
                quantise_kv(k_groups, HEAD_PAIRS if GROUPS - 1 in k_groups else 1)
                for g in k_groups:
                    quantised[g] = n
        second_products(len(turns) + 3, len(passes))
        norms_of_first_batches()
        finish_first_batches()

        for pair in range(HEAD_PAIRS):
            sums = kv_sums[(last_batch, pair)]
            pair_sum_squares = consts.tile([P, 1], F32, name="pair_sum_squares" + str(pair))
            for half in range(2):
                rows = half_rows(half)
                nc.scalar.activation(
                    out=squares[rows, places + pair, :],
                    in_=sums[rows, rows],
                    func=ACT.Square,
                    accum_out=pair_sum_squares[rows, :],
                )
            pair_inverse_norms = consts.tile([P, 1], F32, name="pair_inverse_norms" + str(pair))
            nc.scalar.activation(
                out=pair_inverse_norms[:], in_=pair_sum_squares[:], func=ACT.Abs_reciprocal_sqrt
            )
            pair_result = consts.tile([P, HEAD_DIM], F32, name="pair_result" + str(pair))
            for half in range(2):
                rows = half_rows(half)
                nc.vector.tensor_scalar(
                    out=pair_result[rows, :],
                    in0=sums[rows, rows],
                    scalar1=pair_inverse_norms[rows, :],
                    scalar2=gamma_rows[rows, pair : pair + 1],
                    op0=MULT,
                    op1=MULT,
                )
            nc.sync.dma_start(
                out=out[last_batch, pair * 2 : (pair + 1) * 2].rearrange("half i j -> (half i) j"),
                in_=pair_result[:],
            )
